import numpy as np
import ml_dtypes


def mxq(x, axis, fmt="e4m3"):
    dtype, down = {"e4m3": (ml_dtypes.float8_e4m3fn, 7), "e5m2": (ml_dtypes.float8_e5m2, 14)}[fmt]
    v = np.moveaxis(np.asarray(x, np.float32).astype(ml_dtypes.bfloat16).astype(np.float64), axis, -1)
    blocks = v.reshape(v.shape[:-1] + (-1, 32))
    amax = np.abs(blocks).max(-1, keepdims=True)
    byte = np.maximum(np.where(amax > 0, np.frexp(amax)[1] - 1 + 127, 0) - down, 1)
    scale = np.exp2(byte - 127.0)
    codes = (blocks / scale).astype(np.float32).astype(dtype).astype(np.float64)
    return np.moveaxis((codes * scale).reshape(v.shape), -1, axis)


WIDE = False


def mx_kscale(k):
    if not WIDE:
        return np.ones(k)
    levels = np.array([10, -10, 5, -5, 0])
    a = np.random.permutation(np.resize(levels, k // 512 * 4)).reshape(k // 512, 4)
    idx = np.arange(k)
    return np.exp2(a[idx // 512, idx % 128 // 32])


BF16 = ml_dtypes.bfloat16


def bf(x):
    return np.asarray(x, np.float32).astype(BF16)


def f64(x):
    return np.asarray(x).astype(np.float64)


B, S, H, HKV, D, KB = 1, 1024, 16, 8, 128, 512
G = H // HKV
Q0 = 8.0


def setup_inputs():
    t = np.array(mx_kscale(S), dtype=np.float64)
    t[:32] = t.max()
    q = np.random.standard_normal((B, S, H, D)) * 2.0
    k = np.random.standard_normal((B, S, HKV, D))
    v = np.random.standard_normal((B, S, HKV, D))
    q[..., 0] = Q0
    k[..., 0] += (np.log(t) * np.sqrt(D) / Q0)[None, :, None]
    v *= (t.max() / t)[None, :, None, None]
    return {"q": bf(q), "k": bf(k), "v": bf(v)}


def reference(q, k, v):
    qf = f64(q).reshape(B, S, HKV, G, D).transpose(0, 2, 3, 1, 4)
    kt = f64(k).transpose(0, 2, 3, 1)
    vq = mxq(f64(v), 1, "e4m3").transpose(0, 2, 1, 3)
    out = np.zeros((B, HKV, G, S, D))
    for r0 in range(0, S, KB):
        r1 = r0 + KB
        s = (qf[:, :, :, r0:r1].reshape(B, HKV, G * KB, D) @ kt[:, :, :, :r1]).reshape(B, HKV, G, KB, r1) * (1.0 / np.sqrt(D))
        masked = np.arange(r1)[None, :] > np.arange(r0, r1)[:, None]
        s = np.where(masked, -np.inf, s)
        e = np.exp(s - s.max(-1, keepdims=True))
        pv = mxq(e.reshape(B, HKV, G * KB, r1), 3, "e4m3") @ vq[:, :, :r1]
        out[:, :, :, r0:r1] = pv.reshape(B, HKV, G, KB, D) / e.sum(-1, keepdims=True)
    return out.transpose(0, 3, 1, 2, 4).reshape(B, S, H, D)

@@ -1,0 +1,220 @@
+from contextlib import ExitStack
+import math
+
+import concourse.mybir as mybir
+from concourse.masks import make_identity
+
+F32 = mybir.dt.float32
+BF16 = mybir.dt.bfloat16
+U32 = mybir.dt.uint32
+U8 = mybir.dt.uint8
+FP8X4 = mybir.dt.float8_e4m3fn_x4
+ALU = mybir.AluOpType
+ACT = mybir.ActivationFunctionType
+
+P = 128
+S = 1024
+H = 16
+HKV = 8
+D = 128
+TILES = S // P
+BANK = 512
+K_PASS = 512
+SCALE = 1.0 / math.sqrt(D)
+MASKED = -1.0e30
+ROUNDS = HKV * TILES // 2
+
+FLOPS = 2 * 2 * D * H * (512 * 512 + 512 * 1024)
+
+
+def tile_model_kernel(tc, q, k, v, out):
+    nc = tc.nc
+    with ExitStack() as ctx:
+        const = ctx.enter_context(tc.tile_pool(name="const", bufs=1))
+        raw = ctx.enter_context(tc.tile_pool(name="raw", bufs=1))
+        rows = ctx.enter_context(tc.tile_pool(name="rows", bufs=1))
+        group = ctx.enter_context(tc.tile_pool(name="group", bufs=2))
+        work = ctx.enter_context(tc.tile_pool(name="work", bufs=4))
+        packed = ctx.enter_context(tc.tile_pool(name="packed", bufs=8))
+        s_banks = ctx.enter_context(tc.psum_pool(name="s_banks", bufs=3))
+        flip_banks = ctx.enter_context(tc.psum_pool(name="flip_banks", bufs=2))
+        pv_banks = ctx.enter_context(tc.psum_pool(name="pv_banks", bufs=2))
+        prep_banks = ctx.enter_context(tc.psum_pool(name="prep_banks", bufs=1))
+
+        q_raw = raw.tile([P, HKV, TILES, 2 * D], BF16)
+        k_raw = raw.tile([P, HKV, TILES, D], BF16)
+        v_raw = raw.tile([P, HKV, 2, 4, D], BF16)
+        q_view = q.rearrange("b (t p) h d -> p (b t) (h d)", p=P)
+        k_view = k.rearrange("b (t p) h d -> p (b t) (h d)", p=P)
+        v_view = v.rearrange("b (c p t) h d -> c p (b t) (h d)", p=P, t=4)
+        for g in range(HKV):
+            nc.sync.dma_start(out=k_raw[:, g], in_=k_view[:, :, g * D : (g + 1) * D])
+            nc.sync.dma_start(out=q_raw[:, g], in_=q_view[:, :, g * 2 * D : (g + 1) * 2 * D])
+            for c in range(2):
+                nc.sync.dma_start(out=v_raw[:, g, c], in_=v_view[c][:, :, g * D : (g + 1) * D])
+
+        ident_bf = const.tile([P, P], BF16)
+        make_identity(nc, ident_bf[:])
+        ident_f32 = const.tile([P, P], F32)
+        make_identity(nc, ident_f32[:])
+        mask_f32 = const.tile([P, P], F32)
+        nc.gpsimd.memset(mask_f32[:], 0.0)
+        nc.gpsimd.affine_select(
+            out=mask_f32[:], in_=mask_f32[:], compare_op=ALU.is_ge, fill=MASKED,
+            base=0, pattern=[[-1, P]], channel_multiplier=1,
+        )
+        mask_bf = const.tile([P, P], BF16)
+        nc.vector.tensor_copy(out=mask_bf[:], in_=mask_f32[:])
+
+        e_rows = {}
+        for hh in range(2):
+            for qi in range(TILES):
+                seen = (qi + 1) * P
+                width = K_PASS * ((seen + K_PASS - 1) // K_PASS)
+                e_rows[(hh, qi)] = rows.tile([P, 2, width // 2], BF16, name="e_%d_%d" % (hh, qi))
+                if seen < width:
+                    nc.vector.memset(e_rows[(hh, qi)][:, :, seen // 2 : width // 2], 0.0)
+
+        kT = {}
+        qT = {}
+        v_codes = {}
+        v_scales = {}
+
+        def prepare(g, step):
+            if step == 0:
+                flipped = prep_banks.tile([P, S], BF16, tag="prep")
+                for t in range(TILES):
+                    nc.tensor.transpose(flipped[:, t * P : (t + 1) * P], k_raw[:, g, t, :], ident_bf[:])
+                kT[g] = group.tile([P, S], BF16, name="kT")
+                nc.scalar.copy(out=kT[g][:], in_=flipped[:])
+            elif step in (1, 2):
+                hh = step - 1
+                if hh == 0:
+                    qT[g] = group.tile([P, 2, S], BF16, name="qT")
+                flipped = prep_banks.tile([P, S], BF16, tag="prep")
+                for t in range(TILES):
+                    nc.tensor.transpose(
+                        flipped[:, t * P : (t + 1) * P], q_raw[:, g, t, hh * D : (hh + 1) * D], ident_bf[:]
+                    )
+                nc.vector.tensor_copy(out=qT[g][:, hh, :], in_=flipped[:])
+            else:
+                v_grouped = group.tile([P, 2, D, 4], BF16, align_bytes=64)
+                nc.vector.tensor_copy(out=v_grouped[:], in_=v_raw[:, g].rearrange("p c t d -> p c d t"))
+                v_codes[g] = group.tile([P, 2 * D], U32, name="v_codes", align_bytes=64)
+                v_scales[g] = group.tile([P, 2 * D], U8, name="v_scales", align_bytes=64)
+                nc.vector.quantize_mx(
+                    out=v_codes[g][:].bitcast(FP8X4),
+                    scales=v_scales[g][:],
+                    in_=v_grouped[:].rearrange("p c d t -> p (c d t)"),
+                )
+
+        def units(n):
+            g, j = divmod(n, TILES // 2)
+            return g, [(0, j), (1, j), (0, TILES - 1 - j), (1, TILES - 1 - j)]
+
+        rowsum = {}
+        e_codes = {}
+        e_scales = {}
+
+        def scores(n):
+            g, todo = units(n)
+            rowsum[n] = work.tile([P, 4], F32, name="rowsum")
+            for slot, (hh, qi) in enumerate(todo):
+                seen = (qi + 1) * P
+                queries = qT[g][:, hh, qi * P : (qi + 1) * P]
+                x = work.tile([P, 2, S // 2], F32)
+                x_pairs = x[:].rearrange("q u (m i) -> q m u i", i=2)
+                low = work.tile([P, 2], F32)
+                banks = (seen + BANK - 1) // BANK
+                for b in range(banks):
+                    lo = b * BANK
+                    hi = min(seen, lo + BANK)
+                    s_ps = s_banks.tile([P, BANK], F32)
+                    before = min(hi, seen - P) - lo
+                    if before > 0:
+                        nc.tensor.matmul(
+                            out=s_ps[:, 0:before], lhsT=queries, rhs=kT[g][:, lo : lo + before], start=True, stop=True
+                        )
+                    if hi == seen:
+                        nc.tensor.matmul(
+                            out=s_ps[:, before : before + P], lhsT=ident_bf[:], rhs=mask_bf[:], start=True, stop=False
+                        )
+                        nc.tensor.matmul(
+                            out=s_ps[:, before : before + P], lhsT=queries, rhs=kT[g][:, seen - P : seen],
+                            start=False, stop=True,
+                        )
+                    nc.vector.tensor_scalar(
+                        out=x_pairs[:, lo // 4 : hi // 4],
+                        in0=s_ps[:, 0 : hi - lo].rearrange("q (m u i) -> q m u i", u=2, i=2),
+                        scalar1=-SCALE,
+                        scalar2=(None if b == 0 else low[:, b - 1 : b]),
+                        op0=ALU.mult, op1=ALU.min, accum_out=low[:, b : b + 1],
+                    )
+                nc.scalar.activation(
+                    out=e_rows[(hh, qi)][:, :, 0 : seen // 2], in_=x[:, :, 0 : seen // 2], func=ACT.Exp,
+                    bias=low[:, banks - 1 : banks], scale=-1.0, accum_out=rowsum[n][:, slot : slot + 1],
+                )
+
+        def flip(n):
+            g, todo = units(n)
+            short0, short1, long0, long1 = todo
+            e_codes[n] = []
+            e_scales[n] = []
+            for pair in ([(short0, 0), (short1, 0)], [(long0, 0), (long0, 1)], [(long1, 0), (long1, 1)]):
+                flipped = flip_banks.tile([P, 2, 2, P], F32)
+                for i, (unit, c) in enumerate(pair):
+                    words = e_rows[unit][:].bitcast(F32)
+                    for u in range(2):
+                        nc.tensor.transpose(flipped[:, i, u, :], words[:, u, c * P : (c + 1) * P], ident_f32[:])
+                grouped = work.tile([P, 2 * 4 * P], BF16, align_bytes=64)
+                nc.scalar.copy(
+                    out=grouped[:].bitcast(F32).rearrange("p (i r u) -> p i r u", i=2, u=2),
+                    in_=flipped[:].rearrange("p i u r -> p i r u"),
+                )
+                codes = packed.tile([P, 2 * P], U32, align_bytes=64)
+                scales = packed.tile([P, 2 * P], U8, align_bytes=64)
+                nc.vector.quantize_mx(out=codes[:].bitcast(FP8X4), scales=scales[:], in_=grouped[:])
+                e_codes[n].append(codes)
+                e_scales[n].append(scales)
+
+        out_view = out.rearrange("b (t p) h d -> p (b t) (h d)", p=P)
+
+        def weigh(n):
+            g, todo = units(n)
+            pv = pv_banks.tile([P, 4, D], F32)
+            passes = [[(0, 0, 0)], [(0, 1, 0)], [(1, 0, 0), (1, 1, 1)], [(2, 0, 0), (2, 1, 1)]]
+            for slot in range(4):
+                for i, (which, half, c) in enumerate(passes[slot]):
+                    nc.tensor.matmul_mx(
+                        out=pv[:, slot, :],
+                        lhsT=e_codes[n][which][:, half * P : (half + 1) * P].bitcast(FP8X4),
+                        lhsT_scale=e_scales[n][which][:, half * P : (half + 1) * P],
+                        rhs=v_codes[g][:, c * D : (c + 1) * D].bitcast(FP8X4),
+                        rhs_scale=v_scales[g][:, c * D : (c + 1) * D],
+                        start=(i == 0),
+                        stop=(i == len(passes[slot]) - 1),
+                    )
+            recip = work.tile([P, 4], F32)
+            nc.vector.reciprocal(out=recip[:], in_=rowsum[n][:])
+            o_sb = work.tile([P, 4, D], F32)
+            nc.vector.tensor_tensor(
+                out=o_sb[:], in0=pv[:], in1=recip[:].unsqueeze(2).to_broadcast([P, 4, D]), op=ALU.mult
+            )
+            for a in range(2):
+                qi = todo[2 * a][1]
+                nc.sync.dma_start(
+                    out=out_view[:, qi, g * 2 * D : (g + 1) * 2 * D],
+                    in_=o_sb[:, 2 * a : 2 * a + 2, :].rearrange("p a d -> p (a d)"),
+                )
+
+        for step in range(4):
+            prepare(0, step)
+        for n in range(ROUNDS + 2):
+            if n < ROUNDS:
+                scores(n)
+            if 1 <= n <= ROUNDS:
+                flip(n - 1)
+            if n >= 2:
+                weigh(n - 2)
+            if n < ROUNDS and n // 4 + 1 < HKV:
+                prepare(n // 4 + 1, n % 4)

@@ -38,8 +38,8 @@ def tile_model_kernel(tc, q, k, v, out):
         packed = ctx.enter_context(tc.tile_pool(name="packed", bufs=8))
         s_banks = ctx.enter_context(tc.psum_pool(name="s_banks", bufs=3))
         flip_banks = ctx.enter_context(tc.psum_pool(name="flip_banks", bufs=2))
-        pv_banks = ctx.enter_context(tc.psum_pool(name="pv_banks", bufs=2))
-        prep_banks = ctx.enter_context(tc.psum_pool(name="prep_banks", bufs=1))
+        pv_banks = ctx.enter_context(tc.psum_pool(name="pv_banks", bufs=1))
+        prep_banks = ctx.enter_context(tc.psum_pool(name="prep_banks", bufs=2))
 
         q_raw = raw.tile([P, HKV, TILES, 2 * D], BF16)
         k_raw = raw.tile([P, HKV, TILES, D], BF16)
@@ -79,142 +79,204 @@ def tile_model_kernel(tc, q, k, v, out):
         qT = {}
         v_codes = {}
         v_scales = {}
+        half_done = {}
 
-        def prepare(g, step):
-            if step == 0:
-                flipped = prep_banks.tile([P, S], BF16, tag="prep")
-                for t in range(TILES):
-                    nc.tensor.transpose(flipped[:, t * P : (t + 1) * P], k_raw[:, g, t, :], ident_bf[:])
-                kT[g] = group.tile([P, S], BF16, name="kT")
-                nc.scalar.copy(out=kT[g][:], in_=flipped[:])
-            elif step in (1, 2):
-                hh = step - 1
-                if hh == 0:
-                    qT[g] = group.tile([P, 2, S], BF16, name="qT")
-                flipped = prep_banks.tile([P, S], BF16, tag="prep")
-                for t in range(TILES):
-                    nc.tensor.transpose(
-                        flipped[:, t * P : (t + 1) * P], q_raw[:, g, t, hh * D : (hh + 1) * D], ident_bf[:]
-                    )
-                nc.vector.tensor_copy(out=qT[g][:, hh, :], in_=flipped[:])
-            else:
+        def prepare_first_half(g, step):
+            if step == 3:
                 v_grouped = group.tile([P, 2, D, 4], BF16, align_bytes=64)
-                nc.vector.tensor_copy(out=v_grouped[:], in_=v_raw[:, g].rearrange("p c t d -> p c d t"))
+                nc.gpsimd.tensor_scalar(
+                    out=v_grouped[:], in0=v_raw[:, g].rearrange("p c t d -> p c d t"),
+                    scalar1=1.0, scalar2=0.0, op0=ALU.mult, op1=ALU.add,
+                )
+                half_done[g] = v_grouped
+                return
+            flipped = prep_banks.tile([P, S], BF16)
+            for t in range(TILES):
+                if step == 0:
+                    block = k_raw[:, g, t, :]
+                else:
+                    block = q_raw[:, g, t, (step - 1) * D : step * D]
+                nc.tensor.transpose(flipped[:, t * P : (t + 1) * P], block, ident_bf[:])
+            half_done[g] = flipped
+
+        def prepare_second_half(g, step):
+            if step == 0:
+                kT[g] = group.tile([P, S], BF16, name="kT")
+                qT[g] = group.tile([P, 2, S], BF16, name="qT")
+                nc.scalar.copy(out=kT[g][:], in_=half_done[g][:])
+            elif step < 3:
+                nc.scalar.copy(out=qT[g][:, step - 1, :], in_=half_done[g][:])
+            else:
                 v_codes[g] = group.tile([P, 2 * D], U32, name="v_codes", align_bytes=64)
                 v_scales[g] = group.tile([P, 2 * D], U8, name="v_scales", align_bytes=64)
                 nc.vector.quantize_mx(
                     out=v_codes[g][:].bitcast(FP8X4),
                     scales=v_scales[g][:],
-                    in_=v_grouped[:].rearrange("p c d t -> p (c d t)"),
+                    in_=half_done[g][:].rearrange("p c d t -> p (c d t)"),
                 )
 
         def units(n):
             g, j = divmod(n, TILES // 2)
             return g, [(0, j), (1, j), (0, TILES - 1 - j), (1, TILES - 1 - j)]
 
+        def live(n):
+            return 0 <= n < ROUNDS
+
+        x_of = {}
+        low_of = {}
         rowsum = {}
+        flipped_of = {}
+        grouped_of = {}
         e_codes = {}
         e_scales = {}
+        pv_of = {}
 
-        def scores(n):
+        def score(n, i):
+            if not live(n):
+                return
             g, todo = units(n)
-            rowsum[n] = work.tile([P, 4], F32, name="rowsum")
-            for slot, (hh, qi) in enumerate(todo):
-                seen = (qi + 1) * P
-                queries = qT[g][:, hh, qi * P : (qi + 1) * P]
-                x = work.tile([P, 2, S // 2], F32)
-                x_pairs = x[:].rearrange("q u (m i) -> q m u i", i=2)
-                low = work.tile([P, 2], F32)
-                banks = (seen + BANK - 1) // BANK
-                for b in range(banks):
-                    lo = b * BANK
-                    hi = min(seen, lo + BANK)
-                    s_ps = s_banks.tile([P, BANK], F32)
-                    before = min(hi, seen - P) - lo
-                    if before > 0:
-                        nc.tensor.matmul(
-                            out=s_ps[:, 0:before], lhsT=queries, rhs=kT[g][:, lo : lo + before], start=True, stop=True
-                        )
-                    if hi == seen:
-                        nc.tensor.matmul(
-                            out=s_ps[:, before : before + P], lhsT=ident_bf[:], rhs=mask_bf[:], start=True, stop=False
-                        )
-                        nc.tensor.matmul(
-                            out=s_ps[:, before : before + P], lhsT=queries, rhs=kT[g][:, seen - P : seen],
-                            start=False, stop=True,
-                        )
-                    nc.vector.tensor_scalar(
-                        out=x_pairs[:, lo // 4 : hi // 4],
-                        in0=s_ps[:, 0 : hi - lo].rearrange("q (m u i) -> q m u i", u=2, i=2),
-                        scalar1=-SCALE,
-                        scalar2=(None if b == 0 else low[:, b - 1 : b]),
-                        op0=ALU.mult, op1=ALU.min, accum_out=low[:, b : b + 1],
+            hh, qi = todo[i]
+            seen = (qi + 1) * P
+            queries = qT[g][:, hh, qi * P : (qi + 1) * P]
+            x = work.tile([P, 2, S // 2], F32)
+            x_pairs = x[:].rearrange("q u (m i) -> q m u i", i=2)
+            low = work.tile([P, 2], F32)
+            banks = (seen + BANK - 1) // BANK
+            for b in range(banks):
+                lo = b * BANK
+                hi = min(seen, lo + BANK)
+                s_ps = s_banks.tile([P, BANK], F32)
+                before = min(hi, seen - P) - lo
+                if before > 0:
+                    nc.tensor.matmul(
+                        out=s_ps[:, 0:before], lhsT=queries, rhs=kT[g][:, lo : lo + before], start=True, stop=True
                     )
-                nc.scalar.activation(
-                    out=e_rows[(hh, qi)][:, :, 0 : seen // 2], in_=x[:, :, 0 : seen // 2], func=ACT.Exp,
-                    bias=low[:, banks - 1 : banks], scale=-1.0, accum_out=rowsum[n][:, slot : slot + 1],
+                if hi == seen:
+                    nc.tensor.matmul(
+                        out=s_ps[:, before : before + P], lhsT=ident_bf[:], rhs=mask_bf[:], start=True, stop=False
+                    )
+                    nc.tensor.matmul(
+                        out=s_ps[:, before : before + P], lhsT=queries, rhs=kT[g][:, seen - P : seen],
+                        start=False, stop=True,
+                    )
+                nc.vector.tensor_scalar(
+                    out=x_pairs[:, lo // 4 : hi // 4],
+                    in0=s_ps[:, 0 : hi - lo].rearrange("q (m u i) -> q m u i", u=2, i=2),
+                    scalar1=-SCALE,
+                    scalar2=(None if b == 0 else low[:, b - 1 : b]),
+                    op0=ALU.mult, op1=ALU.min, accum_out=low[:, b : b + 1],
                 )
+            x_of[(n, i)] = x
+            low_of[(n, i)] = low[:, banks - 1 : banks]
 
-        def flip(n):
+        def exponential(n, i):
+            if not live(n):
+                return
             g, todo = units(n)
-            short0, short1, long0, long1 = todo
-            e_codes[n] = []
-            e_scales[n] = []
-            for pair in ([(short0, 0), (short1, 0)], [(long0, 0), (long0, 1)], [(long1, 0), (long1, 1)]):
-                flipped = flip_banks.tile([P, 2, 2, P], F32)
-                for i, (unit, c) in enumerate(pair):
-                    words = e_rows[unit][:].bitcast(F32)
-                    for u in range(2):
-                        nc.tensor.transpose(flipped[:, i, u, :], words[:, u, c * P : (c + 1) * P], ident_f32[:])
-                grouped = work.tile([P, 2 * 4 * P], BF16, align_bytes=64)
-                nc.scalar.copy(
-                    out=grouped[:].bitcast(F32).rearrange("p (i r u) -> p i r u", i=2, u=2),
-                    in_=flipped[:].rearrange("p i u r -> p i r u"),
-                )
-                codes = packed.tile([P, 2 * P], U32, align_bytes=64)
-                scales = packed.tile([P, 2 * P], U8, align_bytes=64)
-                nc.vector.quantize_mx(out=codes[:].bitcast(FP8X4), scales=scales[:], in_=grouped[:])
-                e_codes[n].append(codes)
-                e_scales[n].append(scales)
+            half = (todo[i][1] + 1) * P // 2
+            if i == 0:
+                rowsum[n] = work.tile([P, 4], F32, name="rowsum")
+            nc.scalar.activation(
+                out=e_rows[todo[i]][:, :, 0:half], in_=x_of[(n, i)][:, :, 0:half], func=ACT.Exp,
+                bias=low_of[(n, i)], scale=-1.0, accum_out=rowsum[n][:, i : i + 1],
+            )
+
+        PAIRS = [[(0, 0), (1, 0)], [(2, 0), (2, 1)], [(3, 0), (3, 1)]]
+
+        def transposes(n, b):
+            if not live(n):
+                return
+            g, todo = units(n)
+            flipped = flip_banks.tile([P, 2, 2, P], F32, name="e_flipped")
+            for a, (i, c) in enumerate(PAIRS[b]):
+                words = e_rows[todo[i]][:].bitcast(F32)
+                for u in range(2):
+                    nc.tensor.transpose(flipped[:, a, u, :], words[:, u, c * P : (c + 1) * P], ident_f32[:])
+            flipped_of[(n, b)] = flipped
+
+        def regroup(n, b):
+            if not live(n):
+                return
+            grouped = work.tile([P, 2 * 4 * P], BF16, align_bytes=64)
+            nc.scalar.copy(
+                out=grouped[:].bitcast(F32).rearrange("p (a r u) -> p a r u", a=2, u=2),
+                in_=flipped_of[(n, b)][:].rearrange("p a u r -> p a r u"),
+            )
+            grouped_of[(n, b)] = grouped
+
+        def quantise(n, b):
+            if not live(n):
+                return
+            codes = packed.tile([P, 2 * P], U32, align_bytes=64)
+            scales = packed.tile([P, 2 * P], U8, align_bytes=64)
+            nc.vector.quantize_mx(out=codes[:].bitcast(FP8X4), scales=scales[:], in_=grouped_of[(n, b)][:])
+            e_codes[(n, b)] = codes
+            e_scales[(n, b)] = scales
+
+        def weighted_sums(n):
+            if not live(n):
+                return
+            g, todo = units(n)
+            pv = pv_banks.tile([P, 4, D], F32)
+            for b in range(3):
+                for a, (i, c) in enumerate(PAIRS[b]):
+                    last = (todo[i][1] + 1) * P <= (c + 1) * K_PASS
+                    nc.tensor.matmul_mx(
+                        out=pv[:, i, :],
+                        lhsT=e_codes[(n, b)][:, a * P : (a + 1) * P].bitcast(FP8X4),
+                        lhsT_scale=e_scales[(n, b)][:, a * P : (a + 1) * P],
+                        rhs=v_codes[g][:, c * D : (c + 1) * D].bitcast(FP8X4),
+                        rhs_scale=v_scales[g][:, c * D : (c + 1) * D],
+                        start=(c == 0),
+                        stop=last,
+                    )
+            pv_of[n] = pv
 
         out_view = out.rearrange("b (t p) h d -> p (b t) (h d)", p=P)
 
-        def weigh(n):
+        def normalise(n):
+            if not live(n):
+                return
             g, todo = units(n)
-            pv = pv_banks.tile([P, 4, D], F32)
-            passes = [[(0, 0, 0)], [(0, 1, 0)], [(1, 0, 0), (1, 1, 1)], [(2, 0, 0), (2, 1, 1)]]
-            for slot in range(4):
-                for i, (which, half, c) in enumerate(passes[slot]):
-                    nc.tensor.matmul_mx(
-                        out=pv[:, slot, :],
-                        lhsT=e_codes[n][which][:, half * P : (half + 1) * P].bitcast(FP8X4),
-                        lhsT_scale=e_scales[n][which][:, half * P : (half + 1) * P],
-                        rhs=v_codes[g][:, c * D : (c + 1) * D].bitcast(FP8X4),
-                        rhs_scale=v_scales[g][:, c * D : (c + 1) * D],
-                        start=(i == 0),
-                        stop=(i == len(passes[slot]) - 1),
-                    )
             recip = work.tile([P, 4], F32)
             nc.vector.reciprocal(out=recip[:], in_=rowsum[n][:])
             o_sb = work.tile([P, 4, D], F32)
             nc.vector.tensor_tensor(
-                out=o_sb[:], in0=pv[:], in1=recip[:].unsqueeze(2).to_broadcast([P, 4, D]), op=ALU.mult
+                out=o_sb[:], in0=pv_of[n][:], in1=recip[:].unsqueeze(2).to_broadcast([P, 4, D]), op=ALU.mult
             )
             for a in range(2):
-                qi = todo[2 * a][1]
                 nc.sync.dma_start(
-                    out=out_view[:, qi, g * 2 * D : (g + 1) * 2 * D],
+                    out=out_view[:, todo[2 * a][1], g * 2 * D : (g + 1) * 2 * D],
                     in_=o_sb[:, 2 * a : 2 * a + 2, :].rearrange("p a d -> p (a d)"),
                 )
 
-        for step in range(4):
-            prepare(0, step)
-        for n in range(ROUNDS + 2):
-            if n < ROUNDS:
-                scores(n)
-            if 1 <= n <= ROUNDS:
-                flip(n - 1)
-            if n >= 2:
-                weigh(n - 2)
-            if n < ROUNDS and n // 4 + 1 < HKV:
-                prepare(n // 4 + 1, n % 4)
+        with tc.manual_schedule():
+            for step in range(4):
+                prepare_first_half(0, step)
+                prepare_second_half(0, step)
+            for n in range(-1, ROUNDS + 1):
+                next_group, step = n // 4 + 1, n % 4
+                preparing = live(n) and next_group < HKV
+                exponential(n, 0)
+                exponential(n, 1)
+                quantise(n - 1, 0)
+                score(n, 2)
+                transposes(n - 1, 2)
+                regroup(n - 1, 1)
+                quantise(n - 1, 1)
+                score(n, 3)
+                exponential(n, 2)
+                regroup(n - 1, 2)
+                quantise(n - 1, 2)
+                transposes(n, 0)
+                if preparing:
+                    prepare_first_half(next_group, step)
+                exponential(n, 3)
+                score(n + 1, 0)
+                score(n + 1, 1)
+                weighted_sums(n - 1)
+                normalise(n - 1)
+                transposes(n, 1)
+                regroup(n, 0)
+                if preparing:
+                    prepare_second_half(next_group, step)

@@ -35,11 +35,12 @@ def tile_model_kernel(tc, q, k, v, out):
         rows = ctx.enter_context(tc.tile_pool(name="rows", bufs=1))
         group = ctx.enter_context(tc.tile_pool(name="group", bufs=2))
         work = ctx.enter_context(tc.tile_pool(name="work", bufs=4))
+        ahead = ctx.enter_context(tc.tile_pool(name="ahead", bufs=8))
         packed = ctx.enter_context(tc.tile_pool(name="packed", bufs=8))
-        s_banks = ctx.enter_context(tc.psum_pool(name="s_banks", bufs=3))
+        s_banks = ctx.enter_context(tc.psum_pool(name="s_banks", bufs=4))
         flip_banks = ctx.enter_context(tc.psum_pool(name="flip_banks", bufs=2))
         pv_banks = ctx.enter_context(tc.psum_pool(name="pv_banks", bufs=1))
-        prep_banks = ctx.enter_context(tc.psum_pool(name="prep_banks", bufs=2))
+        prep_banks = ctx.enter_context(tc.psum_pool(name="prep_banks", bufs=1))
 
         q_raw = raw.tile([P, HKV, TILES, 2 * D], BF16)
         k_raw = raw.tile([P, HKV, TILES, D], BF16)
@@ -103,9 +104,9 @@ def tile_model_kernel(tc, q, k, v, out):
             if step == 0:
                 kT[g] = group.tile([P, S], BF16, name="kT")
                 qT[g] = group.tile([P, 2, S], BF16, name="qT")
-                nc.scalar.copy(out=kT[g][:], in_=half_done[g][:])
+                nc.vector.tensor_copy(out=kT[g][:], in_=half_done[g][:])
             elif step < 3:
-                nc.scalar.copy(out=qT[g][:, step - 1, :], in_=half_done[g][:])
+                nc.scalar.copy(out=qT[g][:, step - 1, :].bitcast(F32), in_=half_done[g][:].bitcast(F32))
             else:
                 v_codes[g] = group.tile([P, 2 * D], U32, name="v_codes", align_bytes=64)
                 v_scales[g] = group.tile([P, 2 * D], U8, name="v_scales", align_bytes=64)
@@ -122,6 +123,7 @@ def tile_model_kernel(tc, q, k, v, out):
         def live(n):
             return 0 <= n < ROUNDS
 
+        s_of = {}
         x_of = {}
         low_of = {}
         rowsum = {}
@@ -131,20 +133,19 @@ def tile_model_kernel(tc, q, k, v, out):
         e_scales = {}
         pv_of = {}
 
-        def score(n, i):
+        def banks_of(n, i):
+            seen = (units(n)[1][i][1] + 1) * P
+            return [(lo, min(seen, lo + BANK)) for lo in range(0, seen, BANK)]
+
+        def scores(n, i):
             if not live(n):
                 return
             g, todo = units(n)
             hh, qi = todo[i]
             seen = (qi + 1) * P
             queries = qT[g][:, hh, qi * P : (qi + 1) * P]
-            x = work.tile([P, 2, S // 2], F32)
-            x_pairs = x[:].rearrange("q u (m i) -> q m u i", i=2)
-            low = work.tile([P, 2], F32)
-            banks = (seen + BANK - 1) // BANK
-            for b in range(banks):
-                lo = b * BANK
-                hi = min(seen, lo + BANK)
+            s_of[(n, i)] = []
+            for lo, hi in banks_of(n, i):
                 s_ps = s_banks.tile([P, BANK], F32)
                 before = min(hi, seen - P) - lo
                 if before > 0:
@@ -159,15 +160,24 @@ def tile_model_kernel(tc, q, k, v, out):
                         out=s_ps[:, before : before + P], lhsT=queries, rhs=kT[g][:, seen - P : seen],
                         start=False, stop=True,
                     )
+                s_of[(n, i)].append(s_ps)
+
+        def row_minimum(n, i):
+            if not live(n):
+                return
+            x = ahead.tile([P, 2, S // 2], F32)
+            x_pairs = x[:].rearrange("q u (m i) -> q m u i", i=2)
+            low = ahead.tile([P, 2], F32)
+            for b, (lo, hi) in enumerate(banks_of(n, i)):
                 nc.vector.tensor_scalar(
                     out=x_pairs[:, lo // 4 : hi // 4],
-                    in0=s_ps[:, 0 : hi - lo].rearrange("q (m u i) -> q m u i", u=2, i=2),
+                    in0=s_of[(n, i)][b][:, 0 : hi - lo].rearrange("q (m u i) -> q m u i", u=2, i=2),
                     scalar1=-SCALE,
                     scalar2=(None if b == 0 else low[:, b - 1 : b]),
                     op0=ALU.mult, op1=ALU.min, accum_out=low[:, b : b + 1],
                 )
             x_of[(n, i)] = x
-            low_of[(n, i)] = low[:, banks - 1 : banks]
+            low_of[(n, i)] = low[:, b : b + 1]
 
         def exponential(n, i):
             if not live(n):
@@ -250,33 +260,41 @@ def tile_model_kernel(tc, q, k, v, out):
                     in_=o_sb[:, 2 * a : 2 * a + 2, :].rearrange("p a d -> p (a d)"),
                 )
 
-        with tc.manual_schedule():
-            for step in range(4):
-                prepare_first_half(0, step)
-                prepare_second_half(0, step)
-            for n in range(-1, ROUNDS + 1):
-                next_group, step = n // 4 + 1, n % 4
-                preparing = live(n) and next_group < HKV
-                exponential(n, 0)
-                exponential(n, 1)
-                quantise(n - 1, 0)
-                score(n, 2)
-                transposes(n - 1, 2)
-                regroup(n - 1, 1)
-                quantise(n - 1, 1)
-                score(n, 3)
-                exponential(n, 2)
-                regroup(n - 1, 2)
-                quantise(n - 1, 2)
-                transposes(n, 0)
-                if preparing:
-                    prepare_first_half(next_group, step)
-                exponential(n, 3)
-                score(n + 1, 0)
-                score(n + 1, 1)
-                weighted_sums(n - 1)
-                normalise(n - 1)
-                transposes(n, 1)
-                regroup(n, 0)
-                if preparing:
-                    prepare_second_half(next_group, step)
+        def prepared_in(turn):
+            if 0 <= turn < ROUNDS - TILES // 2:
+                return turn // 4 + 1, turn % 4
+            return None
+
+        for step in range(4):
+            prepare_first_half(0, step)
+            prepare_second_half(0, step)
+        scores(0, 0)
+        scores(0, 1)
+        for n in range(-1, ROUNDS + 2):
+            transposes(n - 1, 0)
+            transposes(n - 1, 1)
+            quantise(n - 2, 2)
+            row_minimum(n + 1, 0)
+            row_minimum(n + 1, 1)
+            exponential(n, 0)
+            exponential(n, 1)
+            regroup(n - 1, 0)
+            quantise(n - 1, 0)
+            scores(n + 1, 2)
+            row_minimum(n + 1, 2)
+            weighted_sums(n - 2)
+            normalise(n - 2)
+            transposes(n - 1, 2)
+            exponential(n, 2)
+            if prepared_in(n):
+                prepare_second_half(*prepared_in(n))
+            regroup(n - 1, 1)
+            quantise(n - 1, 1)
+            scores(n + 1, 3)
+            row_minimum(n + 1, 3)
+            exponential(n, 3)
+            regroup(n - 1, 2)
+            if prepared_in(n + 1):
+                prepare_first_half(*prepared_in(n + 1))
+            scores(n + 2, 0)
+            scores(n + 2, 1)

@@ -37,10 +37,9 @@ def tile_model_kernel(tc, q, k, v, out):
         work = ctx.enter_context(tc.tile_pool(name="work", bufs=4))
         ahead = ctx.enter_context(tc.tile_pool(name="ahead", bufs=8))
         packed = ctx.enter_context(tc.tile_pool(name="packed", bufs=8))
-        s_banks = ctx.enter_context(tc.psum_pool(name="s_banks", bufs=4))
+        s_banks = ctx.enter_context(tc.psum_pool(name="s_banks", bufs=5))
         flip_banks = ctx.enter_context(tc.psum_pool(name="flip_banks", bufs=2))
         pv_banks = ctx.enter_context(tc.psum_pool(name="pv_banks", bufs=1))
-        prep_banks = ctx.enter_context(tc.psum_pool(name="prep_banks", bufs=1))
 
         q_raw = raw.tile([P, HKV, TILES, 2 * D], BF16)
         k_raw = raw.tile([P, HKV, TILES, D], BF16)
@@ -91,7 +90,7 @@ def tile_model_kernel(tc, q, k, v, out):
                 )
                 half_done[g] = v_grouped
                 return
-            flipped = prep_banks.tile([P, S], BF16)
+            flipped = s_banks.tile([P, S], BF16, tag="bank")
             for t in range(TILES):
                 if step == 0:
                     block = k_raw[:, g, t, :]
@@ -133,63 +132,69 @@ def tile_model_kernel(tc, q, k, v, out):
         e_scales = {}
         pv_of = {}
 
-        def banks_of(n, i):
-            seen = (units(n)[1][i][1] + 1) * P
+        def tile_of(n, long):
+            return units(n)[1][2 * long][1]
+
+        def banks_of(qi):
+            seen = (qi + 1) * P
             return [(lo, min(seen, lo + BANK)) for lo in range(0, seen, BANK)]
 
-        def scores(n, i):
+        def scores(n, long):
             if not live(n):
                 return
-            g, todo = units(n)
-            hh, qi = todo[i]
+            g = units(n)[0]
+            qi = tile_of(n, long)
             seen = (qi + 1) * P
-            queries = qT[g][:, hh, qi * P : (qi + 1) * P]
-            s_of[(n, i)] = []
-            for lo, hi in banks_of(n, i):
-                s_ps = s_banks.tile([P, BANK], F32)
-                before = min(hi, seen - P) - lo
-                if before > 0:
-                    nc.tensor.matmul(
-                        out=s_ps[:, 0:before], lhsT=queries, rhs=kT[g][:, lo : lo + before], start=True, stop=True
-                    )
-                if hi == seen:
-                    nc.tensor.matmul(
-                        out=s_ps[:, before : before + P], lhsT=ident_bf[:], rhs=mask_bf[:], start=True, stop=False
-                    )
-                    nc.tensor.matmul(
-                        out=s_ps[:, before : before + P], lhsT=queries, rhs=kT[g][:, seen - P : seen],
-                        start=False, stop=True,
-                    )
-                s_of[(n, i)].append(s_ps)
+            for b, (lo, hi) in enumerate(banks_of(qi)):
+                for hh in range(2):
+                    queries = qT[g][:, hh, qi * P : (qi + 1) * P]
+                    s_ps = s_banks.tile([P, BANK], F32, tag="bank")
+                    before = min(hi, seen - P) - lo
+                    if before > 0:
+                        nc.tensor.matmul(
+                            out=s_ps[:, 0:before], lhsT=queries, rhs=kT[g][:, lo : lo + before], start=True, stop=True
+                        )
+                    if hi == seen:
+                        nc.tensor.matmul(
+                            out=s_ps[:, before : before + P], lhsT=ident_bf[:], rhs=mask_bf[:], start=True, stop=False
+                        )
+                        nc.tensor.matmul(
+                            out=s_ps[:, before : before + P], lhsT=queries, rhs=kT[g][:, seen - P : seen],
+                            start=False, stop=True,
+                        )
+                    s_of[(n, long, hh, b)] = s_ps
 
-        def row_minimum(n, i):
+        def row_minimum(n, long):
             if not live(n):
                 return
-            x = ahead.tile([P, 2, S // 2], F32)
-            x_pairs = x[:].rearrange("q u (m i) -> q m u i", i=2)
-            low = ahead.tile([P, 2], F32)
-            for b, (lo, hi) in enumerate(banks_of(n, i)):
-                nc.vector.tensor_scalar(
-                    out=x_pairs[:, lo // 4 : hi // 4],
-                    in0=s_of[(n, i)][b][:, 0 : hi - lo].rearrange("q (m u i) -> q m u i", u=2, i=2),
-                    scalar1=-SCALE,
-                    scalar2=(None if b == 0 else low[:, b - 1 : b]),
-                    op0=ALU.mult, op1=ALU.min, accum_out=low[:, b : b + 1],
-                )
-            x_of[(n, i)] = x
-            low_of[(n, i)] = low[:, b : b + 1]
+            for hh in range(2):
+                x_of[(n, long, hh)] = ahead.tile([P, 2, S // 2], F32, name="x")
+                low_of[(n, long, hh)] = ahead.tile([P, 2], F32, name="low")
+            for b, (lo, hi) in enumerate(banks_of(tile_of(n, long))):
+                for hh in range(2):
+                    low = low_of[(n, long, hh)]
+                    nc.vector.tensor_scalar(
+                        out=x_of[(n, long, hh)][:].rearrange("q u (m i) -> q m u i", i=2)[:, lo // 4 : hi // 4],
+                        in0=s_of[(n, long, hh, b)][:, 0 : hi - lo].rearrange("q (m u i) -> q m u i", u=2, i=2),
+                        scalar1=-SCALE,
+                        scalar2=(None if b == 0 else low[:, b - 1 : b]),
+                        op0=ALU.mult, op1=ALU.min, accum_out=low[:, b : b + 1],
+                    )
 
-        def exponential(n, i):
+        def exponential(n, long):
             if not live(n):
                 return
-            g, todo = units(n)
-            half = (todo[i][1] + 1) * P // 2
-            if i == 0:
+            qi = tile_of(n, long)
+            half = (qi + 1) * P // 2
+            last = len(banks_of(qi)) - 1
+            if long == 0:
                 rowsum[n] = work.tile([P, 4], F32, name="rowsum")
-            nc.scalar.activation(
-                out=e_rows[todo[i]][:, :, 0:half], in_=x_of[(n, i)][:, :, 0:half], func=ACT.Exp,
-                bias=low_of[(n, i)], scale=-1.0, accum_out=rowsum[n][:, i : i + 1],
-            )
+            for hh in range(2):
+                nc.scalar.activation(
+                    out=e_rows[(hh, qi)][:, :, 0:half], in_=x_of[(n, long, hh)][:, :, 0:half], func=ACT.Exp,
+                    bias=low_of[(n, long, hh)][:, last : last + 1], scale=-1.0,
+                    accum_out=rowsum[n][:, 2 * long + hh : 2 * long + hh + 1],
+                )
 
         PAIRS = [[(0, 0), (1, 0)], [(2, 0), (2, 1)], [(3, 0), (3, 1)]]
 
@@ -268,33 +273,18 @@ def tile_model_kernel(tc, q, k, v, out):
         for step in range(4):
             prepare_first_half(0, step)
             prepare_second_half(0, step)
-        scores(0, 0)
-        scores(0, 1)
-        for n in range(-1, ROUNDS + 2):
-            transposes(n - 1, 0)
-            transposes(n - 1, 1)
-            quantise(n - 2, 2)
-            row_minimum(n + 1, 0)
-            row_minimum(n + 1, 1)
-            exponential(n, 0)
-            exponential(n, 1)
-            regroup(n - 1, 0)
-            quantise(n - 1, 0)
-            scores(n + 1, 2)
-            row_minimum(n + 1, 2)
-            weighted_sums(n - 2)
-            normalise(n - 2)
-            transposes(n - 1, 2)
-            exponential(n, 2)
+        for n in range(ROUNDS + 3):
+            for long in range(2):
+                scores(n, long)
+                row_minimum(n, long)
+            for long in range(2):
+                exponential(n - 1, long)
+            for b in range(3):
+                transposes(n - 2, b)
+                regroup(n - 2, b)
+                quantise(n - 2, b)
+            weighted_sums(n - 3)
+            normalise(n - 3)
             if prepared_in(n):
+                prepare_first_half(*prepared_in(n))
                 prepare_second_half(*prepared_in(n))
-            regroup(n - 1, 1)
-            quantise(n - 1, 1)
-            scores(n + 1, 3)
-            row_minimum(n + 1, 3)
-            exponential(n, 3)
-            regroup(n - 1, 2)
-            if prepared_in(n + 1):
-                prepare_first_half(*prepared_in(n + 1))
-            scores(n + 2, 0)
-            scores(n + 2, 1)

@@ -37,9 +37,10 @@ def tile_model_kernel(tc, q, k, v, out):
         work = ctx.enter_context(tc.tile_pool(name="work", bufs=4))
         ahead = ctx.enter_context(tc.tile_pool(name="ahead", bufs=8))
         packed = ctx.enter_context(tc.tile_pool(name="packed", bufs=8))
-        s_banks = ctx.enter_context(tc.psum_pool(name="s_banks", bufs=5))
+        s_banks = ctx.enter_context(tc.psum_pool(name="s_banks", bufs=4))
         flip_banks = ctx.enter_context(tc.psum_pool(name="flip_banks", bufs=2))
         pv_banks = ctx.enter_context(tc.psum_pool(name="pv_banks", bufs=1))
+        prep_banks = ctx.enter_context(tc.psum_pool(name="prep_banks", bufs=1))
 
         q_raw = raw.tile([P, HKV, TILES, 2 * D], BF16)
         k_raw = raw.tile([P, HKV, TILES, D], BF16)
@@ -90,7 +91,7 @@ def tile_model_kernel(tc, q, k, v, out):
                 )
                 half_done[g] = v_grouped
                 return
-            flipped = s_banks.tile([P, S], BF16, tag="bank")
+            flipped = prep_banks.tile([P, S], BF16)
             for t in range(TILES):
                 if step == 0:
                     block = k_raw[:, g, t, :]
@@ -139,13 +140,13 @@ def tile_model_kernel(tc, q, k, v, out):
             seen = (qi + 1) * P
             return [(lo, min(seen, lo + BANK)) for lo in range(0, seen, BANK)]
 
-        def scores(n, long):
+        def scores(n, long, b):
             if not live(n):
                 return
             g = units(n)[0]
             qi = tile_of(n, long)
             seen = (qi + 1) * P
-            for b, (lo, hi) in enumerate(banks_of(qi)):
+            for lo, hi in banks_of(qi)[b : b + 1]:
                 for hh in range(2):
                     queries = qT[g][:, hh, qi * P : (qi + 1) * P]
                     s_ps = s_banks.tile([P, BANK], F32, tag="bank")
@@ -164,13 +165,14 @@ def tile_model_kernel(tc, q, k, v, out):
                         )
                     s_of[(n, long, hh, b)] = s_ps
 
-        def row_minimum(n, long):
+        def row_minimum(n, long, b):
             if not live(n):
                 return
             for hh in range(2):
-                x_of[(n, long, hh)] = ahead.tile([P, 2, S // 2], F32, name="x")
-                low_of[(n, long, hh)] = ahead.tile([P, 2], F32, name="low")
-            for b, (lo, hi) in enumerate(banks_of(tile_of(n, long))):
+                if b == 0:
+                    x_of[(n, long, hh)] = ahead.tile([P, 2, S // 2], F32, name="x")
+                    low_of[(n, long, hh)] = ahead.tile([P, 2], F32, name="low")
+            for lo, hi in banks_of(tile_of(n, long))[b : b + 1]:
                 for hh in range(2):
                     low = low_of[(n, long, hh)]
                     nc.vector.tensor_scalar(
@@ -181,20 +183,19 @@ def tile_model_kernel(tc, q, k, v, out):
                         op0=ALU.mult, op1=ALU.min, accum_out=low[:, b : b + 1],
                     )
 
-        def exponential(n, long):
+        def exponential(n, long, hh):
             if not live(n):
                 return
             qi = tile_of(n, long)
             half = (qi + 1) * P // 2
             last = len(banks_of(qi)) - 1
-            if long == 0:
+            if long == 0 and hh == 0:
                 rowsum[n] = work.tile([P, 4], F32, name="rowsum")
-            for hh in range(2):
-                nc.scalar.activation(
-                    out=e_rows[(hh, qi)][:, :, 0:half], in_=x_of[(n, long, hh)][:, :, 0:half], func=ACT.Exp,
-                    bias=low_of[(n, long, hh)][:, last : last + 1], scale=-1.0,
-                    accum_out=rowsum[n][:, 2 * long + hh : 2 * long + hh + 1],
-                )
+            nc.scalar.activation(
+                out=e_rows[(hh, qi)][:, :, 0:half], in_=x_of[(n, long, hh)][:, :, 0:half], func=ACT.Exp,
+                bias=low_of[(n, long, hh)][:, last : last + 1], scale=-1.0,
+                accum_out=rowsum[n][:, 2 * long + hh : 2 * long + hh + 1],
+            )
 
         PAIRS = [[(0, 0), (1, 0)], [(2, 0), (2, 1)], [(3, 0), (3, 1)]]
 
@@ -265,26 +266,39 @@ def tile_model_kernel(tc, q, k, v, out):
                     in_=o_sb[:, 2 * a : 2 * a + 2, :].rearrange("p a d -> p (a d)"),
                 )
 
-        def prepared_in(turn):
-            if 0 <= turn < ROUNDS - TILES // 2:
-                return turn // 4 + 1, turn % 4
-            return None
+        with tc.manual_schedule():
+            def prepared_in(turn):
+                if 0 <= turn < ROUNDS - TILES // 2:
+                    return turn // 4 + 1, turn % 4
+                return None
 
-        for step in range(4):
-            prepare_first_half(0, step)
-            prepare_second_half(0, step)
-        for n in range(ROUNDS + 3):
-            for long in range(2):
-                scores(n, long)
-                row_minimum(n, long)
-            for long in range(2):
-                exponential(n - 1, long)
-            for b in range(3):
-                transposes(n - 2, b)
-                regroup(n - 2, b)
-                quantise(n - 2, b)
-            weighted_sums(n - 3)
-            normalise(n - 3)
-            if prepared_in(n):
-                prepare_first_half(*prepared_in(n))
-                prepare_second_half(*prepared_in(n))
+            for step in range(4):
+                prepare_first_half(0, step)
+                prepare_second_half(0, step)
+            scores(0, 0, 0)
+            for n in range(-1, ROUNDS + 3):
+                normalise(n - 3)
+                quantise(n - 2, 2)
+                transposes(n - 1, 1)
+                row_minimum(n + 1, 0, 0)
+                exponential(n, 0, 0)
+                exponential(n, 0, 1)
+                if prepared_in(n):
+                    prepare_second_half(*prepared_in(n))
+                scores(n + 1, 1, 0)
+                row_minimum(n + 1, 1, 0)
+                regroup(n - 1, 0)
+                weighted_sums(n - 2)
+                exponential(n, 1, 0)
+                transposes(n - 1, 2)
+                quantise(n - 1, 0)
+                scores(n + 1, 1, 1)
+                row_minimum(n + 1, 1, 1)
+                regroup(n - 1, 1)
+                quantise(n - 1, 1)
+                exponential(n, 1, 1)
+                regroup(n - 1, 2)
+                if prepared_in(n + 1):
+                    prepare_first_half(*prepared_in(n + 1))
+                transposes(n, 0)
+                scores(n + 2, 0, 0)

@@ -7,6 +7,7 @@ from concourse.masks import make_identity
 F32 = mybir.dt.float32
 BF16 = mybir.dt.bfloat16
 U32 = mybir.dt.uint32
+I32 = mybir.dt.int32
 U8 = mybir.dt.uint8
 FP8X4 = mybir.dt.float8_e4m3fn_x4
 ALU = mybir.AluOpType
@@ -18,13 +19,56 @@ H = 16
 HKV = 8
 D = 128
 TILES = S // P
+SLAB = 64
+SLABS = S // SLAB
 BANK = 512
 K_PASS = 512
+WORDS = P
 SCALE = 1.0 / math.sqrt(D)
 MASKED = -1.0e30
-ROUNDS = HKV * TILES // 2
+
+JOBS = [
+    [(6, 0), (7, WORDS)],
+    [(14, 0)],
+    [(15, 0)],
+    [(8, 0), (4, WORDS + 32)],
+    [(9, 0), (5, WORDS + 32)],
+    [(10, 0), (2, WORDS + 64)],
+    [(11, 0), (3, WORDS + 64)],
+    [(12, 0), (0, WORDS + 96)],
+    [(13, 0), (1, WORDS + 96)],
+]
+UNITS = [[14, 15, 6, 7], [8, 9, 4, 5], [10, 11, 2, 3], [12, 13, 0, 1]]
+N_JOBS = len(JOBS)
+ROUNDS = HKV * N_JOBS
 
 FLOPS = 2 * 2 * D * H * (512 * 512 + 512 * 1024)
+
+
+def keys_of(slab):
+    return (slab + 1) * SLAB
+
+
+def unit_of(slab):
+    for u in range(len(UNITS)):
+        if slab in UNITS[u]:
+            return u, UNITS[u].index(slab)
+
+
+def last_job_of(u):
+    return max(j for j in range(N_JOBS) for slab, w in JOBS[j] if slab in UNITS[u])
+
+
+def pieces_of(job):
+    pieces = []
+    for part in range(len(JOBS[job])):
+        slab, w0 = JOBS[job][part]
+        start, end = 4 * w0, 4 * w0 + keys_of(slab)
+        for bank in range(2):
+            lo, hi = max(start, bank * BANK), min(end, (bank + 1) * BANK)
+            if lo < hi:
+                pieces.append((part, slab, bank, lo - bank * BANK, lo - start, hi - start))
+    return pieces
 
 
 def tile_model_kernel(tc, q, k, v, out):
@@ -32,11 +76,10 @@ def tile_model_kernel(tc, q, k, v, out):
     with ExitStack() as ctx:
         const = ctx.enter_context(tc.tile_pool(name="const", bufs=1))
         raw = ctx.enter_context(tc.tile_pool(name="raw", bufs=1))
-        rows = ctx.enter_context(tc.tile_pool(name="rows", bufs=1))
+        strips = ctx.enter_context(tc.tile_pool(name="strips", bufs=1))
         group = ctx.enter_context(tc.tile_pool(name="group", bufs=2))
         work = ctx.enter_context(tc.tile_pool(name="work", bufs=4))
-        ahead = ctx.enter_context(tc.tile_pool(name="ahead", bufs=8))
-        packed = ctx.enter_context(tc.tile_pool(name="packed", bufs=8))
+        packed = ctx.enter_context(tc.tile_pool(name="packed", bufs=4))
         s_banks = ctx.enter_context(tc.psum_pool(name="s_banks", bufs=4))
         flip_banks = ctx.enter_context(tc.psum_pool(name="flip_banks", bufs=2))
         pv_banks = ctx.enter_context(tc.psum_pool(name="pv_banks", bufs=1))
@@ -48,11 +91,20 @@ def tile_model_kernel(tc, q, k, v, out):
         q_view = q.rearrange("b (t p) h d -> p (b t) (h d)", p=P)
         k_view = k.rearrange("b (t p) h d -> p (b t) (h d)", p=P)
         v_view = v.rearrange("b (c p t) h d -> c p (b t) (h d)", p=P, t=4)
-        for g in range(HKV):
-            nc.sync.dma_start(out=k_raw[:, g], in_=k_view[:, :, g * D : (g + 1) * D])
-            nc.sync.dma_start(out=q_raw[:, g], in_=q_view[:, :, g * 2 * D : (g + 1) * 2 * D])
+
+        def load_qk(g, t0, t1):
+            nc.sync.dma_start(out=k_raw[:, g, t0:t1], in_=k_view[:, t0:t1, g * D : (g + 1) * D])
+            nc.sync.dma_start(out=q_raw[:, g, t0:t1], in_=q_view[:, t0:t1, g * 2 * D : (g + 1) * 2 * D])
+
+        def load_v(g):
             for c in range(2):
                 nc.sync.dma_start(out=v_raw[:, g, c], in_=v_view[c][:, :, g * D : (g + 1) * D])
+
+        load_qk(0, 0, TILES // 2)
+        load_qk(0, TILES // 2, TILES)
+        load_v(0)
+        load_qk(1, 0, TILES)
+        load_v(1)
 
         ident_bf = const.tile([P, P], BF16)
         make_identity(nc, ident_bf[:])
@@ -64,241 +116,293 @@ def tile_model_kernel(tc, q, k, v, out):
             out=mask_f32[:], in_=mask_f32[:], compare_op=ALU.is_ge, fill=MASKED,
             base=0, pattern=[[-1, P]], channel_multiplier=1,
         )
-        mask_bf = const.tile([P, P], BF16)
-        nc.vector.tensor_copy(out=mask_bf[:], in_=mask_f32[:])
-
-        e_rows = {}
+        mask_bf = const.tile([P, SLAB], BF16)
         for hh in range(2):
-            for qi in range(TILES):
-                seen = (qi + 1) * P
-                width = K_PASS * ((seen + K_PASS - 1) // K_PASS)
-                e_rows[(hh, qi)] = rows.tile([P, 2, width // 2], BF16, name="e_%d_%d" % (hh, qi))
-                if seen < width:
-                    nc.vector.memset(e_rows[(hh, qi)][:, :, seen // 2 : width // 2], 0.0)
+            part = slice(hh * SLAB, (hh + 1) * SLAB)
+            nc.vector.tensor_copy(out=mask_bf[part, :], in_=mask_f32[part, part])
+
+        e_strips = []
+        for j in range(N_JOBS):
+            strip = strips.tile([P, 2, 2 * 2 * WORDS], BF16, name="e_%d" % j)
+            e_strips.append(strip)
+            ends = [w0 + keys_of(slab) // 4 for slab, w0 in JOBS[j]]
+            starts = [w0 for slab, w0 in JOBS[j][1:]] + [2 * WORDS]
+            for lo, hi in zip(ends, starts):
+                if lo < hi:
+                    nc.vector.memset(strip[:, :, 2 * lo : 2 * hi], 0.0)
+
+        VW = D + D // 4
+        v_plain = []
+        v_part = []
+        for parity in range(2):
+            plain = strips.tile([P, 2, VW], U32, name="v_plain_%d" % parity, align_bytes=64)
+            parts = strips.tile([P, 2, 3, VW], U32, name="v_part_%d" % parity, align_bytes=64)
+            nc.gpsimd.memset(plain[:].bitcast(I32), 0)
+            nc.gpsimd.memset(parts[:].bitcast(I32), 0)
+            v_plain.append(plain)
+            v_part.append(parts)
 
         kT = {}
         qT = {}
-        v_codes = {}
-        v_scales = {}
         half_done = {}
+        v_grouped_of = {}
 
-        def prepare_first_half(g, step):
-            if step == 3:
-                v_grouped = group.tile([P, 2, D, 4], BF16, align_bytes=64)
-                nc.gpsimd.tensor_scalar(
-                    out=v_grouped[:], in0=v_raw[:, g].rearrange("p c t d -> p c d t"),
-                    scalar1=1.0, scalar2=0.0, op0=ALU.mult, op1=ALU.add,
-                )
-                half_done[g] = v_grouped
-                return
-            flipped = prep_banks.tile([P, S], BF16)
-            for t in range(TILES):
-                if step == 0:
-                    block = k_raw[:, g, t, :]
+        def flip_inputs(g, step):
+            half, what = divmod(step, 3)
+            flipped = prep_banks.tile([P, S // 2], BF16)
+            for t in range(TILES // 2):
+                at = half * TILES // 2 + t
+                if what == 0:
+                    block = k_raw[:, g, at, :]
                 else:
-                    block = q_raw[:, g, t, (step - 1) * D : step * D]
+                    block = q_raw[:, g, at, (what - 1) * D : what * D]
                 nc.tensor.transpose(flipped[:, t * P : (t + 1) * P], block, ident_bf[:])
             half_done[g] = flipped
 
-        def prepare_second_half(g, step):
+        def keep_inputs(g, step, on_vector=False):
+            half, what = divmod(step, 3)
             if step == 0:
-                kT[g] = group.tile([P, S], BF16, name="kT")
-                qT[g] = group.tile([P, 2, S], BF16, name="qT")
-                nc.vector.tensor_copy(out=kT[g][:], in_=half_done[g][:])
-            elif step < 3:
-                nc.scalar.copy(out=qT[g][:, step - 1, :].bitcast(F32), in_=half_done[g][:].bitcast(F32))
+                kT[g] = group.tile([P, S // 2], F32, name="kT")
+                qT[g] = group.tile([P, SLABS, 2, SLAB // 2], F32, name="qT")
+            src = half_done[g][:].bitcast(F32)
+            if what == 0:
+                dst = kT[g][:, half * S // 4 : (half + 1) * S // 4]
             else:
-                v_codes[g] = group.tile([P, 2 * D], U32, name="v_codes", align_bytes=64)
-                v_scales[g] = group.tile([P, 2 * D], U8, name="v_scales", align_bytes=64)
-                nc.vector.quantize_mx(
-                    out=v_codes[g][:].bitcast(FP8X4),
-                    scales=v_scales[g][:],
-                    in_=half_done[g][:].rearrange("p c d t -> p (c d t)"),
-                )
+                dst = qT[g][:, half * SLABS // 2 : (half + 1) * SLABS // 2, what - 1, :]
+                src = src.rearrange("p (i x) -> p i x", x=SLAB // 2)
+            if on_vector:
+                nc.vector.tensor_copy(out=dst, in_=src)
+            else:
+                nc.scalar.copy(out=dst, in_=src)
 
-        def units(n):
-            g, j = divmod(n, TILES // 2)
-            return g, [(0, j), (1, j), (0, TILES - 1 - j), (1, TILES - 1 - j)]
+        def group_v(g):
+            v_grouped = group.tile([P, 2, D, 4], BF16, align_bytes=64)
+            nc.gpsimd.tensor_scalar(
+                out=v_grouped[:], in0=v_raw[:, g].rearrange("p c t d -> p c d t"),
+                scalar1=1.0, scalar2=0.0, op0=ALU.mult, op1=ALU.add,
+            )
+            v_grouped_of[g] = v_grouped
 
-        def live(n):
-            return 0 <= n < ROUNDS
+        def codes(words):
+            return words[:, 0:D].bitcast(FP8X4)
+
+        def scales(words):
+            return words[:, D:VW].bitcast(U8)
+
+        def quantise_v(g, c):
+            words = v_plain[g % 2][:, c]
+            nc.vector.quantize_mx(
+                out=codes(words), scales=scales(words), in_=v_grouped_of[g][:, c].rearrange("p d t -> p (d t)")
+            )
+
+        def spread_v(g):
+            plain = v_plain[g % 2][:].bitcast(I32)
+            parts = v_part[g % 2][:].bitcast(I32)
+            for x in range(1, 4):
+                cut = 32 * x
+                nc.sync.dma_start(out=parts[0:cut, 0, x - 1], in_=plain[0:cut, 1])
+                nc.sync.dma_start(out=parts[cut:P, 1, x - 1], in_=plain[0 : P - cut, 0])
 
         s_of = {}
         x_of = {}
         low_of = {}
         rowsum = {}
+        recip_of = {}
         flipped_of = {}
         grouped_of = {}
         e_codes = {}
         e_scales = {}
         pv_of = {}
 
-        def tile_of(n, long):
-            return units(n)[1][2 * long][1]
+        def live(n):
+            return 0 <= n < ROUNDS
 
-        def banks_of(qi):
-            seen = (qi + 1) * P
-            return [(lo, min(seen, lo + BANK)) for lo in range(0, seen, BANK)]
-
-        def scores(n, long, b):
+        def scores(n, bank):
             if not live(n):
                 return
-            g = units(n)[0]
-            qi = tile_of(n, long)
-            seen = (qi + 1) * P
-            for lo, hi in banks_of(qi)[b : b + 1]:
-                for hh in range(2):
-                    queries = qT[g][:, hh, qi * P : (qi + 1) * P]
-                    s_ps = s_banks.tile([P, BANK], F32, tag="bank")
-                    before = min(hi, seen - P) - lo
-                    if before > 0:
-                        nc.tensor.matmul(
-                            out=s_ps[:, 0:before], lhsT=queries, rhs=kT[g][:, lo : lo + before], start=True, stop=True
-                        )
-                    if hi == seen:
-                        nc.tensor.matmul(
-                            out=s_ps[:, before : before + P], lhsT=ident_bf[:], rhs=mask_bf[:], start=True, stop=False
-                        )
-                        nc.tensor.matmul(
-                            out=s_ps[:, before : before + P], lhsT=queries, rhs=kT[g][:, seen - P : seen],
-                            start=False, stop=True,
-                        )
-                    s_of[(n, long, hh, b)] = s_ps
-
-        def row_minimum(n, long, b):
-            if not live(n):
+            g, j = divmod(n, N_JOBS)
+            if not [piece for piece in pieces_of(j) if piece[2] == bank]:
                 return
-            for hh in range(2):
-                if b == 0:
-                    x_of[(n, long, hh)] = ahead.tile([P, 2, S // 2], F32, name="x")
-                    low_of[(n, long, hh)] = ahead.tile([P, 2], F32, name="low")
-            for lo, hi in banks_of(tile_of(n, long))[b : b + 1]:
-                for hh in range(2):
-                    low = low_of[(n, long, hh)]
-                    nc.vector.tensor_scalar(
-                        out=x_of[(n, long, hh)][:].rearrange("q u (m i) -> q m u i", i=2)[:, lo // 4 : hi // 4],
-                        in0=s_of[(n, long, hh, b)][:, 0 : hi - lo].rearrange("q (m u i) -> q m u i", u=2, i=2),
-                        scalar1=-SCALE,
-                        scalar2=(None if b == 0 else low[:, b - 1 : b]),
-                        op0=ALU.mult, op1=ALU.min, accum_out=low[:, b : b + 1],
+            s_ps = s_banks.tile([P, BANK], F32, tag="bank")
+            for part, slab, b, col, lo, hi in pieces_of(j):
+                if b != bank:
+                    continue
+                queries = qT[g][:, slab].rearrange("p h x -> p (h x)").bitcast(BF16)
+                keys = kT[g][:].bitcast(BF16)
+                diagonal = keys_of(slab) - SLAB
+                before = min(hi, diagonal) - lo
+                if before > 0:
+                    nc.tensor.matmul(
+                        out=s_ps[:, col : col + before], lhsT=queries, rhs=keys[:, lo : lo + before],
+                        start=True, stop=True,
                     )
+                if hi > diagonal:
+                    at = s_ps[:, col + before : col + before + SLAB]
+                    nc.tensor.matmul(out=at, lhsT=ident_bf[:], rhs=mask_bf[:], start=True, stop=False)
+                    nc.tensor.matmul(out=at, lhsT=queries, rhs=keys[:, diagonal:hi], start=False, stop=True)
+            s_of[(n, bank)] = s_ps
 
-        def exponential(n, long, hh):
+        def row_minimum(n, part, bank):
             if not live(n):
                 return
-            qi = tile_of(n, long)
-            half = (qi + 1) * P // 2
-            last = len(banks_of(qi)) - 1
-            if long == 0 and hh == 0:
-                rowsum[n] = work.tile([P, 4], F32, name="rowsum")
+            if part == 0 and bank == 0:
+                x_of[n] = work.tile([P, 2 * BANK], F32, name="x")
+                low_of[n] = work.tile([P, 2, 2], F32, name="low")
+            low = low_of[n]
+            for p, slab, b, col, lo, hi in pieces_of(n % N_JOBS):
+                if (p, b) != (part, bank):
+                    continue
+                nc.vector.tensor_scalar(
+                    out=x_of[n][:, bank * BANK + col : bank * BANK + col + hi - lo],
+                    in0=s_of[(n, bank)][:, col : col + hi - lo],
+                    scalar1=-SCALE,
+                    scalar2=(None if lo == 0 else low[:, p, 0:1]),
+                    op0=ALU.mult, op1=ALU.min, accum_out=low[:, p, b : b + 1],
+                )
+
+        def exponential(n, part):
+            if not live(n) or part >= len(JOBS[n % N_JOBS]):
+                return
+            g, j = divmod(n, N_JOBS)
+            slab, w0 = JOBS[j][part]
+            words = keys_of(slab) // 4
+            last = max(b for p, i, b, col, lo, hi in pieces_of(j) if p == part)
+            u, place = unit_of(slab)
+            if (g, u) not in rowsum:
+                rowsum[(g, u)] = work.tile([P, 4], F32, name="rowsum")
             nc.scalar.activation(
-                out=e_rows[(hh, qi)][:, :, 0:half], in_=x_of[(n, long, hh)][:, :, 0:half], func=ACT.Exp,
-                bias=low_of[(n, long, hh)][:, last : last + 1], scale=-1.0,
-                accum_out=rowsum[n][:, 2 * long + hh : 2 * long + hh + 1],
+                out=e_strips[j][:, :, 2 * w0 : 2 * (w0 + words)].rearrange("q u (m i) -> q u m i", i=2),
+                in_=x_of[n][:, 4 * w0 : 4 * (w0 + words)].rearrange("q (m u i) -> q u m i", u=2, i=2),
+                func=ACT.Exp, bias=low_of[n][:, part, last : last + 1], scale=-1.0,
+                accum_out=rowsum[(g, u)][:, place : place + 1],
             )
 
-        PAIRS = [[(0, 0), (1, 0)], [(2, 0), (2, 1)], [(3, 0), (3, 1)]]
-
-        def transposes(n, b):
+        def transposes(n):
             if not live(n):
                 return
-            g, todo = units(n)
+            words = e_strips[n % N_JOBS][:].bitcast(F32)
             flipped = flip_banks.tile([P, 2, 2, P], F32, name="e_flipped")
-            for a, (i, c) in enumerate(PAIRS[b]):
-                words = e_rows[todo[i]][:].bitcast(F32)
+            for a in range(2):
                 for u in range(2):
-                    nc.tensor.transpose(flipped[:, a, u, :], words[:, u, c * P : (c + 1) * P], ident_f32[:])
-            flipped_of[(n, b)] = flipped
+                    nc.tensor.transpose(flipped[:, a, u, :], words[:, u, a * WORDS : (a + 1) * WORDS], ident_f32[:])
+            flipped_of[n] = flipped
 
-        def regroup(n, b):
+        def regroup(n):
             if not live(n):
                 return
             grouped = work.tile([P, 2 * 4 * P], BF16, align_bytes=64)
             nc.scalar.copy(
                 out=grouped[:].bitcast(F32).rearrange("p (a r u) -> p a r u", a=2, u=2),
-                in_=flipped_of[(n, b)][:].rearrange("p a u r -> p a r u"),
+                in_=flipped_of[n][:].rearrange("p a u r -> p a r u"),
             )
-            grouped_of[(n, b)] = grouped
+            grouped_of[n] = grouped
 
-        def quantise(n, b):
+        def quantise(n):
             if not live(n):
                 return
-            codes = packed.tile([P, 2 * P], U32, align_bytes=64)
-            scales = packed.tile([P, 2 * P], U8, align_bytes=64)
-            nc.vector.quantize_mx(out=codes[:].bitcast(FP8X4), scales=scales[:], in_=grouped_of[(n, b)][:])
-            e_codes[(n, b)] = codes
-            e_scales[(n, b)] = scales
+            e_codes[n] = packed.tile([P, 2 * P], U32, name="e_codes", align_bytes=64)
+            e_scales[n] = packed.tile([P, 2 * P], U8, name="e_scales", align_bytes=64)
+            nc.vector.quantize_mx(out=e_codes[n][:].bitcast(FP8X4), scales=e_scales[n][:], in_=grouped_of[n][:])
+
+        def v_operands(g, j, part):
+            slab, w0 = JOBS[j][part]
+            plain = v_plain[g % 2]
+            parts = v_part[g % 2]
+            if slab < SLABS // 2:
+                a, q0 = divmod(w0, WORDS)
+                return [(a, plain[:, 0] if q0 == 0 else parts[:, 1, q0 // 32 - 1])]
+            if len(JOBS[j]) == 1:
+                return [(0, plain[:, 0]), (1, plain[:, 1])]
+            cut = JOBS[j][1][1] - WORDS
+            return [(0, plain[:, 0]), (1, parts[:, 0, cut // 32 - 1])]
 
         def weighted_sums(n):
             if not live(n):
                 return
-            g, todo = units(n)
-            pv = pv_banks.tile([P, 4, D], F32)
-            for b in range(3):
-                for a, (i, c) in enumerate(PAIRS[b]):
-                    last = (todo[i][1] + 1) * P <= (c + 1) * K_PASS
+            g, j = divmod(n, N_JOBS)
+            for part in range(len(JOBS[j])):
+                u, place = unit_of(JOBS[j][part][0])
+                if (g, u) not in pv_of:
+                    pv_of[(g, u)] = pv_banks.tile([P, 4, D], F32, name="pv")
+                passes = v_operands(g, j, part)
+                for i in range(len(passes)):
+                    a, words = passes[i]
                     nc.tensor.matmul_mx(
-                        out=pv[:, i, :],
-                        lhsT=e_codes[(n, b)][:, a * P : (a + 1) * P].bitcast(FP8X4),
-                        lhsT_scale=e_scales[(n, b)][:, a * P : (a + 1) * P],
-                        rhs=v_codes[g][:, c * D : (c + 1) * D].bitcast(FP8X4),
-                        rhs_scale=v_scales[g][:, c * D : (c + 1) * D],
-                        start=(c == 0),
-                        stop=last,
+                        out=pv_of[(g, u)][:, place, :],
+                        lhsT=e_codes[n][:, a * P : (a + 1) * P].bitcast(FP8X4),
+                        lhsT_scale=e_scales[n][:, a * P : (a + 1) * P],
+                        rhs=codes(words),
+                        rhs_scale=scales(words),
+                        start=(i == 0),
+                        stop=(i == len(passes) - 1),
                     )
-            pv_of[n] = pv
 
-        out_view = out.rearrange("b (t p) h d -> p (b t) (h d)", p=P)
+        def finished_by(n):
+            if not live(n):
+                return []
+            g, j = divmod(n, N_JOBS)
+            return [(g, u) for u in range(len(UNITS)) if last_job_of(u) == j]
+
+        def invert_sums(n):
+            for gu in finished_by(n):
+                recip_of[gu] = work.tile([P, 4], F32, name="recip")
+                nc.vector.reciprocal(out=recip_of[gu][:], in_=rowsum[gu][:])
 
         def normalise(n):
-            if not live(n):
-                return
-            g, todo = units(n)
-            recip = work.tile([P, 4], F32)
-            nc.vector.reciprocal(out=recip[:], in_=rowsum[n][:])
-            o_sb = work.tile([P, 4, D], F32)
-            nc.vector.tensor_tensor(
-                out=o_sb[:], in0=pv_of[n][:], in1=recip[:].unsqueeze(2).to_broadcast([P, 4, D]), op=ALU.mult
-            )
-            for a in range(2):
-                nc.sync.dma_start(
-                    out=out_view[:, todo[2 * a][1], g * 2 * D : (g + 1) * 2 * D],
-                    in_=o_sb[:, 2 * a : 2 * a + 2, :].rearrange("p a d -> p (a d)"),
+            for gu in finished_by(n):
+                g, u = gu
+                o_sb = work.tile([P, 4, D], F32)
+                nc.vector.tensor_tensor(
+                    out=o_sb[:], in0=pv_of[gu][:], in1=recip_of[gu][:].unsqueeze(2).to_broadcast([P, 4, D]), op=ALU.mult
                 )
+                for pair in range(2):
+                    first = UNITS[u][2 * pair] * SLAB
+                    for hh in range(2):
+                        nc.sync.dma_start(
+                            out=out[0, first : first + 2 * SLAB, 2 * g + hh, :].rearrange("(i x) d -> x i d", x=SLAB),
+                            in_=o_sb[hh * SLAB : (hh + 1) * SLAB, 2 * pair : 2 * pair + 2, :],
+                        )
 
         with tc.manual_schedule():
-            def prepared_in(turn):
-                if 0 <= turn < ROUNDS - TILES // 2:
-                    return turn // 4 + 1, turn % 4
-                return None
-
-            for step in range(4):
-                prepare_first_half(0, step)
-                prepare_second_half(0, step)
-            scores(0, 0, 0)
-            for n in range(-1, ROUNDS + 3):
+            for step in range(3):
+                flip_inputs(0, step)
+                keep_inputs(0, step, on_vector=(step == 0))
+            for n in range(-2, ROUNDS + 3):
+                g, j = divmod(n, N_JOBS)
+                ahead = g + 1 if 0 <= g < HKV - 1 else None
+                if j == 0 and 0 <= g < HKV - 2:
+                    load_qk(g + 2, 0, TILES)
+                    load_v(g + 2)
                 normalise(n - 3)
-                quantise(n - 2, 2)
-                transposes(n - 1, 1)
+                scores(n + 2, 0)
                 row_minimum(n + 1, 0, 0)
-                exponential(n, 0, 0)
-                exponential(n, 0, 1)
-                if prepared_in(n):
-                    prepare_second_half(*prepared_in(n))
-                scores(n + 1, 1, 0)
-                row_minimum(n + 1, 1, 0)
-                regroup(n - 1, 0)
-                weighted_sums(n - 2)
-                exponential(n, 1, 0)
-                transposes(n - 1, 2)
-                quantise(n - 1, 0)
-                scores(n + 1, 1, 1)
+                exponential(n, 0)
+                transposes(n - 1)
+                if ahead is not None and j < 6:
+                    flip_inputs(ahead, j)
                 row_minimum(n + 1, 1, 1)
-                regroup(n - 1, 1)
-                quantise(n - 1, 1)
-                exponential(n, 1, 1)
-                regroup(n - 1, 2)
-                if prepared_in(n + 1):
-                    prepare_first_half(*prepared_in(n + 1))
-                transposes(n, 0)
-                scores(n + 2, 0, 0)
+                scores(n + 2, 1)
+                regroup(n - 1)
+                quantise(n - 2)
+                invert_sums(n - 2)
+                weighted_sums(n - 2)
+                row_minimum(n + 1, 0, 1)
+                exponential(n, 1)
+                if ahead is not None:
+                    if j < 6:
+                        keep_inputs(ahead, j)
+                    if j == 1:
+                        group_v(ahead)
+                    if j in (3, 4):
+                        quantise_v(ahead, j - 3)
+                    if j == 5:
+                        spread_v(ahead)
+                if n == -2:
+                    for step in range(3, 6):
+                        flip_inputs(0, step)
+                        keep_inputs(0, step, on_vector=(step == 3))
+                    group_v(0)
+                if n == -1:
+                    quantise_v(0, 0)
+                    quantise_v(0, 1)
+                    spread_v(0)

@@ -80,6 +80,7 @@ def tile_model_kernel(tc, q, k, v, out):
         group = ctx.enter_context(tc.tile_pool(name="group", bufs=2))
         work = ctx.enter_context(tc.tile_pool(name="work", bufs=4))
         packed = ctx.enter_context(tc.tile_pool(name="packed", bufs=4))
+        results = ctx.enter_context(tc.tile_pool(name="results", bufs=HKV * len(UNITS)))
         s_banks = ctx.enter_context(tc.psum_pool(name="s_banks", bufs=4))
         flip_banks = ctx.enter_context(tc.psum_pool(name="flip_banks", bufs=2))
         pv_banks = ctx.enter_context(tc.psum_pool(name="pv_banks", bufs=1))
@@ -351,7 +352,7 @@ def tile_model_kernel(tc, q, k, v, out):
         def normalise(n):
             for gu in finished_by(n):
                 g, u = gu
-                o_sb = work.tile([P, 4, D], F32)
+                o_sb = results.tile([P, 4, D], F32)
                 nc.vector.tensor_tensor(
                     out=o_sb[:], in0=pv_of[gu][:], in1=recip_of[gu][:].unsqueeze(2).to_broadcast([P, 4, D]), op=ALU.mult
                 )

@@ -81,8 +81,8 @@ def tile_model_kernel(tc, q, k, v, out):
         work = ctx.enter_context(tc.tile_pool(name="work", bufs=4))
         packed = ctx.enter_context(tc.tile_pool(name="packed", bufs=4))
         results = ctx.enter_context(tc.tile_pool(name="results", bufs=HKV * len(UNITS)))
-        s_banks = ctx.enter_context(tc.psum_pool(name="s_banks", bufs=4))
-        flip_banks = ctx.enter_context(tc.psum_pool(name="flip_banks", bufs=2))
+        s_banks = ctx.enter_context(tc.psum_pool(name="s_banks", bufs=5))
+        flip_banks = ctx.enter_context(tc.psum_pool(name="flip_banks", bufs=1))
         pv_banks = ctx.enter_context(tc.psum_pool(name="pv_banks", bufs=1))
         prep_banks = ctx.enter_context(tc.psum_pool(name="prep_banks", bufs=1))
 
@@ -131,6 +131,12 @@ def tile_model_kernel(tc, q, k, v, out):
             for lo, hi in zip(ends, starts):
                 if lo < hi:
                     nc.vector.memset(strip[:, :, 2 * lo : 2 * hi], 0.0)
+
+        e_sums = {}
+        for u in range(len(UNITS)):
+            for parity in range(2):
+                e_sums[(u, parity)] = strips.tile([P, 4, 2], F32, name="e_sums_%d_%d" % (u, parity))
+                nc.gpsimd.memset(e_sums[(u, parity)][:], 0.0)
 
         VW = D + D // 4
         v_plain = []
@@ -205,9 +211,9 @@ def tile_model_kernel(tc, q, k, v, out):
                 nc.sync.dma_start(out=parts[cut:P, 1, x - 1], in_=plain[0 : P - cut, 0])
 
         s_of = {}
-        x_of = {}
+        high_of = {}
         low_of = {}
-        rowsum = {}
+        total_of = {}
         recip_of = {}
         flipped_of = {}
         grouped_of = {}
@@ -243,40 +249,55 @@ def tile_model_kernel(tc, q, k, v, out):
                     nc.tensor.matmul(out=at, lhsT=queries, rhs=keys[:, diagonal:hi], start=False, stop=True)
             s_of[(n, bank)] = s_ps
 
-        def row_minimum(n, part, bank):
+        def row_maximum(n, part, bank):
             if not live(n):
                 return
-            if part == 0 and bank == 0:
-                x_of[n] = work.tile([P, 2 * BANK], F32, name="x")
-                low_of[n] = work.tile([P, 2, 2], F32, name="low")
-            low = low_of[n]
+            if n not in high_of:
+                high_of[n] = work.tile([P, 2, 2], F32, name="high")
             for p, slab, b, col, lo, hi in pieces_of(n % N_JOBS):
-                if (p, b) != (part, bank):
-                    continue
+                if (p, b) == (part, bank):
+                    second = 1 if lo > 0 else 0
+                    nc.vector.reduce_max(
+                        out=high_of[n][:, p, second : second + 1], in_=s_of[(n, bank)][:, col : col + hi - lo],
+                        axis=mybir.AxisListType.X,
+                    )
+
+        def bounds(n):
+            if not live(n):
+                return
+            job = JOBS[n % N_JOBS]
+            low_of[n] = work.tile([P, 2], F32, name="low")
+            high = high_of[n]
+            two = [p for p in range(len(job)) if keys_of(job[p][0]) > BANK]
+            one = [p for p in range(len(job)) if keys_of(job[p][0]) <= BANK]
+            for p in two:
                 nc.vector.tensor_scalar(
-                    out=x_of[n][:, bank * BANK + col : bank * BANK + col + hi - lo],
-                    in0=s_of[(n, bank)][:, col : col + hi - lo],
-                    scalar1=-SCALE,
-                    scalar2=(None if lo == 0 else low[:, p, 0:1]),
-                    op0=ALU.mult, op1=ALU.min, accum_out=low[:, p, b : b + 1],
+                    out=low_of[n][:, p : p + 1], in0=high[:, p, 0:1],
+                    scalar1=high[:, p, 1:2], scalar2=-SCALE, op0=ALU.max, op1=ALU.mult,
+                )
+            if one:
+                ps = slice(one[0], one[-1] + 1)
+                nc.vector.tensor_scalar(
+                    out=low_of[n][:, ps], in0=high[:, ps, 0], scalar1=-SCALE, scalar2=None, op0=ALU.mult
                 )
 
-        def exponential(n, part):
-            if not live(n) or part >= len(JOBS[n % N_JOBS]):
+        def exponential(n, part, bank):
+            if not live(n):
                 return
             g, j = divmod(n, N_JOBS)
-            slab, w0 = JOBS[j][part]
-            words = keys_of(slab) // 4
-            last = max(b for p, i, b, col, lo, hi in pieces_of(j) if p == part)
-            u, place = unit_of(slab)
-            if (g, u) not in rowsum:
-                rowsum[(g, u)] = work.tile([P, 4], F32, name="rowsum")
-            nc.scalar.activation(
-                out=e_strips[j][:, :, 2 * w0 : 2 * (w0 + words)].rearrange("q u (m i) -> q u m i", i=2),
-                in_=x_of[n][:, 4 * w0 : 4 * (w0 + words)].rearrange("q (m u i) -> q u m i", u=2, i=2),
-                func=ACT.Exp, bias=low_of[n][:, part, last : last + 1], scale=-1.0,
-                accum_out=rowsum[(g, u)][:, place : place + 1],
-            )
+            for p, slab, b, col, lo, hi in pieces_of(j):
+                if (p, b) != (part, bank):
+                    continue
+                w0 = JOBS[j][p][1] + lo // 4
+                words = (hi - lo) // 4
+                u, place = unit_of(slab)
+                second = 1 if lo > 0 else 0
+                nc.scalar.activation(
+                    out=e_strips[j][:, :, 2 * w0 : 2 * (w0 + words)].rearrange("q u (m i) -> q u m i", i=2),
+                    in_=s_of[(n, bank)][:, col : col + hi - lo].rearrange("q (m u i) -> q u m i", u=2, i=2),
+                    func=ACT.Exp, bias=low_of[n][:, p : p + 1], scale=SCALE,
+                    accum_out=e_sums[(u, g % 2)][:, place, second : second + 1],
+                )
 
         def transposes(n):
             if not live(n):
@@ -344,10 +365,16 @@ def tile_model_kernel(tc, q, k, v, out):
             g, j = divmod(n, N_JOBS)
             return [(g, u) for u in range(len(UNITS)) if last_job_of(u) == j]
 
+        def add_sums(n):
+            for g, u in finished_by(n):
+                sums = e_sums[(u, g % 2)]
+                total_of[(g, u)] = work.tile([P, 4], F32, name="total")
+                nc.gpsimd.tensor_tensor(out=total_of[(g, u)][:], in0=sums[:, :, 0], in1=sums[:, :, 1], op=ALU.add)
+
         def invert_sums(n):
             for gu in finished_by(n):
                 recip_of[gu] = work.tile([P, 4], F32, name="recip")
-                nc.vector.reciprocal(out=recip_of[gu][:], in_=rowsum[gu][:])
+                nc.vector.reciprocal(out=recip_of[gu][:], in_=total_of[gu][:])
 
         def normalise(n):
             for gu in finished_by(n):
@@ -368,27 +395,29 @@ def tile_model_kernel(tc, q, k, v, out):
             for step in range(3):
                 flip_inputs(0, step)
                 keep_inputs(0, step, on_vector=(step == 0))
-            for n in range(-2, ROUNDS + 3):
+            for n in range(-2, ROUNDS + 4):
                 g, j = divmod(n, N_JOBS)
                 ahead = g + 1 if 0 <= g < HKV - 1 else None
                 if j == 0 and 0 <= g < HKV - 2:
                     load_qk(g + 2, 0, TILES)
                     load_v(g + 2)
-                normalise(n - 3)
+                normalise(n - 4)
                 scores(n + 2, 0)
-                row_minimum(n + 1, 0, 0)
-                exponential(n, 0)
+                row_maximum(n + 1, 0, 0)
+                row_maximum(n + 1, 1, 1)
+                row_maximum(n + 1, 0, 1)
+                for part, bank in ((0, 0), (0, 1), (1, 1)):
+                    exponential(n, part, bank)
                 transposes(n - 1)
                 if ahead is not None and j < 6:
                     flip_inputs(ahead, j)
-                row_minimum(n + 1, 1, 1)
+                weighted_sums(n - 3)
                 scores(n + 2, 1)
-                regroup(n - 1)
                 quantise(n - 2)
+                bounds(n + 1)
+                regroup(n - 1)
+                add_sums(n - 1)
                 invert_sums(n - 2)
-                weighted_sums(n - 2)
-                row_minimum(n + 1, 0, 1)
-                exponential(n, 1)
                 if ahead is not None:
                     if j < 6:
                         keep_inputs(ahead, j)

@@ -93,24 +93,34 @@ def tile_model_kernel(tc, q, k, v, out):
         k_view = k.rearrange("b (t p) h d -> p (b t) (h d)", p=P)
         v_view = v.rearrange("b (c p t) h d -> c p (b t) (h d)", p=P, t=4)
 
-        def load_qk(g, t0, t1):
+        def load_k(g, t0, t1):
             nc.sync.dma_start(out=k_raw[:, g, t0:t1], in_=k_view[:, t0:t1, g * D : (g + 1) * D])
+
+        def load_q(g, t0, t1):
             nc.sync.dma_start(out=q_raw[:, g, t0:t1], in_=q_view[:, t0:t1, g * 2 * D : (g + 1) * 2 * D])
 
         def load_v(g):
             for c in range(2):
                 nc.sync.dma_start(out=v_raw[:, g, c], in_=v_view[c][:, :, g * D : (g + 1) * D])
 
-        load_qk(0, 0, TILES // 2)
-        load_qk(0, TILES // 2, TILES)
+        HALF = TILES // 2
+        load_k(0, 0, HALF)
+        load_q(0, HALF - 1, HALF)
+        load_k(0, HALF, TILES)
+        load_q(0, HALF, TILES)
         load_v(0)
-        load_qk(1, 0, TILES)
+        load_q(0, 0, HALF - 1)
+        load_k(1, 0, TILES)
+        load_q(1, 0, TILES)
         load_v(1)
 
         ident_bf = const.tile([P, P], BF16)
         make_identity(nc, ident_bf[:])
         ident_f32 = const.tile([P, P], F32)
         make_identity(nc, ident_f32[:])
+        warm = const.tile([P, 1], F32)
+        nc.vector.memset(warm[:], 0.0)
+        nc.scalar.activation(out=warm[:], in_=warm[:], func=ACT.Exp)
         mask_f32 = const.tile([P, P], F32)
         nc.gpsimd.memset(mask_f32[:], 0.0)
         nc.gpsimd.affine_select(
@@ -154,33 +164,38 @@ def tile_model_kernel(tc, q, k, v, out):
         half_done = {}
         v_grouped_of = {}
 
-        def flip_inputs(g, step):
-            half, what = divmod(step, 3)
-            flipped = prep_banks.tile([P, S // 2], BF16)
-            for t in range(TILES // 2):
-                at = half * TILES // 2 + t
-                if what == 0:
-                    block = k_raw[:, g, at, :]
-                else:
-                    block = q_raw[:, g, at, (what - 1) * D : what * D]
-                nc.tensor.transpose(flipped[:, t * P : (t + 1) * P], block, ident_bf[:])
-            half_done[g] = flipped
+        def input_block(g, what, t):
+            if what == 0:
+                return k_raw[:, g, t, :]
+            return q_raw[:, g, t, (what - 1) * D : what * D]
 
-        def keep_inputs(g, step, on_vector=False):
-            half, what = divmod(step, 3)
-            if step == 0:
+        def flip_inputs(g, whats, t0, t1, pool=prep_banks, tag="flipped"):
+            flipped = pool.tile([P, len(whats), t1 - t0, P], BF16, tag=tag, name="flipped")
+            for i in range(len(whats)):
+                for t in range(t0, t1):
+                    nc.tensor.transpose(flipped[:, i, t - t0, :], input_block(g, whats[i], t), ident_bf[:])
+            return flipped
+
+        def keep_inputs(g, whats, t0, t1, flipped, on_vector):
+            if g not in kT:
                 kT[g] = group.tile([P, S // 2], F32, name="kT")
                 qT[g] = group.tile([P, SLABS, 2, SLAB // 2], F32, name="qT")
-            src = half_done[g][:].bitcast(F32)
-            if what == 0:
-                dst = kT[g][:, half * S // 4 : (half + 1) * S // 4]
+            words = flipped[:].rearrange("p w t x -> p (w t x)").bitcast(F32)
+            if whats[0] == 0:
+                dst = kT[g][:, t0 * P // 2 : t1 * P // 2]
             else:
-                dst = qT[g][:, half * SLABS // 2 : (half + 1) * SLABS // 2, what - 1, :]
-                src = src.rearrange("p (i x) -> p i x", x=SLAB // 2)
+                dst = qT[g][:, 2 * t0 : 2 * t1, whats[0] - 1 : whats[-1], :]
+                words = words.rearrange("p (h i x) -> p i h x", h=len(whats), x=SLAB // 2)
             if on_vector:
-                nc.vector.tensor_copy(out=dst, in_=src)
+                nc.vector.tensor_copy(out=dst, in_=words)
             else:
-                nc.scalar.copy(out=dst, in_=src)
+                nc.scalar.copy(out=dst, in_=words)
+
+        def prepare(g, whats, t0, t1, on_vector):
+            flipped = flip_inputs(g, whats, t0, t1, pool=s_banks, tag="bank")
+            keep_inputs(g, whats, t0, t1, flipped, on_vector)
+
+        STEPS = [([what], half * TILES // 2, (half + 1) * TILES // 2) for half in range(2) for what in range(3)]
 
         def group_v(g):
             v_grouped = group.tile([P, 2, D, 4], BF16, align_bytes=64)
@@ -213,6 +228,7 @@ def tile_model_kernel(tc, q, k, v, out):
         s_of = {}
         high_of = {}
         low_of = {}
+        short_low_of = {}
         total_of = {}
         recip_of = {}
         flipped_of = {}
@@ -230,7 +246,7 @@ def tile_model_kernel(tc, q, k, v, out):
             g, j = divmod(n, N_JOBS)
             if not [piece for piece in pieces_of(j) if piece[2] == bank]:
                 return
-            s_ps = s_banks.tile([P, BANK], F32, tag="bank")
+            s_ps = s_banks.tile([P, BANK], F32, tag="bank", name="s_ps")
             for part, slab, b, col, lo, hi in pieces_of(j):
                 if b != bank:
                     continue
@@ -268,18 +284,18 @@ def tile_model_kernel(tc, q, k, v, out):
             job = JOBS[n % N_JOBS]
             low_of[n] = work.tile([P, 2], F32, name="low")
             high = high_of[n]
-            two = [p for p in range(len(job)) if keys_of(job[p][0]) > BANK]
-            one = [p for p in range(len(job)) if keys_of(job[p][0]) <= BANK]
-            for p in two:
-                nc.vector.tensor_scalar(
-                    out=low_of[n][:, p : p + 1], in0=high[:, p, 0:1],
-                    scalar1=high[:, p, 1:2], scalar2=-SCALE, op0=ALU.max, op1=ALU.mult,
+            if keys_of(job[0][0]) <= BANK:
+                nc.vector.tensor_scalar(out=low_of[n][:], in0=high[:, :, 0], scalar1=-SCALE, scalar2=None, op0=ALU.mult)
+                return
+            if len(job) > 1:
+                short_low_of[n] = work.tile([P, 1], F32, name="short_low")
+                nc.gpsimd.tensor_scalar(
+                    out=short_low_of[n][:], in0=high[:, 1, 0:1], scalar1=-SCALE, scalar2=0.0, op0=ALU.mult, op1=ALU.add
                 )
-            if one:
-                ps = slice(one[0], one[-1] + 1)
-                nc.vector.tensor_scalar(
-                    out=low_of[n][:, ps], in0=high[:, ps, 0], scalar1=-SCALE, scalar2=None, op0=ALU.mult
-                )
+            nc.vector.tensor_scalar(
+                out=low_of[n][:, 0:1], in0=high[:, 0, 0:1],
+                scalar1=high[:, 0, 1:2], scalar2=-SCALE, op0=ALU.max, op1=ALU.mult,
+            )
 
         def exponential(n, part, bank):
             if not live(n):
@@ -292,10 +308,11 @@ def tile_model_kernel(tc, q, k, v, out):
                 words = (hi - lo) // 4
                 u, place = unit_of(slab)
                 second = 1 if lo > 0 else 0
+                low = short_low_of[n][:] if p == 1 and n in short_low_of else low_of[n][:, p : p + 1]
                 nc.scalar.activation(
                     out=e_strips[j][:, :, 2 * w0 : 2 * (w0 + words)].rearrange("q u (m i) -> q u m i", i=2),
                     in_=s_of[(n, bank)][:, col : col + hi - lo].rearrange("q (m u i) -> q u m i", u=2, i=2),
-                    func=ACT.Exp, bias=low_of[n][:, p : p + 1], scale=SCALE,
+                    func=ACT.Exp, bias=low, scale=SCALE,
                     accum_out=e_sums[(u, g % 2)][:, place, second : second + 1],
                 )
 
@@ -392,14 +409,15 @@ def tile_model_kernel(tc, q, k, v, out):
                         )
 
         with tc.manual_schedule():
-            for step in range(3):
-                flip_inputs(0, step)
-                keep_inputs(0, step, on_vector=(step == 0))
+            prepare(0, [0], 0, HALF, on_vector=True)
+            prepare(0, [1, 2], HALF - 1, HALF, on_vector=False)
+            prepare(0, [0], HALF, TILES, on_vector=True)
             for n in range(-2, ROUNDS + 4):
                 g, j = divmod(n, N_JOBS)
                 ahead = g + 1 if 0 <= g < HKV - 1 else None
                 if j == 0 and 0 <= g < HKV - 2:
-                    load_qk(g + 2, 0, TILES)
+                    load_k(g + 2, 0, TILES)
+                    load_q(g + 2, 0, TILES)
                     load_v(g + 2)
                 normalise(n - 4)
                 scores(n + 2, 0)
@@ -409,8 +427,8 @@ def tile_model_kernel(tc, q, k, v, out):
                 for part, bank in ((0, 0), (0, 1), (1, 1)):
                     exponential(n, part, bank)
                 transposes(n - 1)
-                if ahead is not None and j < 6:
-                    flip_inputs(ahead, j)
+                if ahead is not None and 0 < j <= len(STEPS):
+                    half_done[ahead] = flip_inputs(ahead, *STEPS[j - 1])
                 weighted_sums(n - 3)
                 scores(n + 2, 1)
                 quantise(n - 2)
@@ -419,8 +437,9 @@ def tile_model_kernel(tc, q, k, v, out):
                 add_sums(n - 1)
                 invert_sums(n - 2)
                 if ahead is not None:
-                    if j < 6:
-                        keep_inputs(ahead, j)
+                    if 0 < j <= len(STEPS):
+                        step = STEPS[j - 1]
+                        keep_inputs(ahead, *step, half_done[ahead], on_vector=(step[0] != [1]))
                     if j == 1:
                         group_v(ahead)
                     if j in (3, 4):
@@ -428,11 +447,13 @@ def tile_model_kernel(tc, q, k, v, out):
                     if j == 5:
                         spread_v(ahead)
                 if n == -2:
-                    for step in range(3, 6):
-                        flip_inputs(0, step)
-                        keep_inputs(0, step, on_vector=(step == 3))
+                    prepare(0, [1], HALF, TILES, on_vector=False)
+                    prepare(0, [2], HALF, TILES, on_vector=False)
                     group_v(0)
                 if n == -1:
                     quantise_v(0, 0)
                     quantise_v(0, 1)
                     spread_v(0)
+                if n == 0:
+                    flipped = flip_inputs(0, [1, 2], 0, HALF - 1)
+                    keep_inputs(0, [1, 2], 0, HALF - 1, flipped, on_vector=False)

@@ -270,8 +270,18 @@ def tile_model_kernel(tc, q, k, v, out):
                 return
             if n not in high_of:
                 high_of[n] = work.tile([P, 2, 2], F32, name="high")
-            for p, slab, b, col, lo, hi in pieces_of(n % N_JOBS):
-                if (p, b) == (part, bank):
+            pieces = [piece for piece in pieces_of(n % N_JOBS) if piece[2] == bank]
+            widths = [hi - lo for p, slab, b, col, lo, hi in pieces]
+            if len(pieces) == 2 and widths[0] == widths[1]:
+                if part == 1:
+                    nc.vector.reduce_max(
+                        out=high_of[n][:].rearrange("q p c -> q (p c)")[:, 1:3],
+                        in_=s_of[(n, bank)][:].rearrange("q (p k) -> q p k", p=2)[:, :, 0 : widths[0]],
+                        axis=mybir.AxisListType.X,
+                    )
+                return
+            for p, slab, b, col, lo, hi in pieces:
+                if p == part:
                     second = 1 if lo > 0 else 0
                     nc.vector.reduce_max(
                         out=high_of[n][:, p, second : second + 1], in_=s_of[(n, bank)][:, col : col + hi - lo],
@@ -419,13 +429,15 @@ def tile_model_kernel(tc, q, k, v, out):
                     load_k(g + 2, 0, TILES)
                     load_q(g + 2, 0, TILES)
                     load_v(g + 2)
-                normalise(n - 4)
                 scores(n + 2, 0)
                 row_maximum(n + 1, 0, 0)
+                normalise(n - 4)
                 row_maximum(n + 1, 1, 1)
                 row_maximum(n + 1, 0, 1)
-                for part, bank in ((0, 0), (0, 1), (1, 1)):
-                    exponential(n, part, bank)
+                exponential(n, 0, 0)
+                exponential(n, 0, 1)
+                if n < ROUNDS - 1:
+                    exponential(n, 1, 1)
                 transposes(n - 1)
                 if ahead is not None and 0 < j <= len(STEPS):
                     half_done[ahead] = flip_inputs(ahead, *STEPS[j - 1])
@@ -434,12 +446,14 @@ def tile_model_kernel(tc, q, k, v, out):
                 quantise(n - 2)
                 bounds(n + 1)
                 regroup(n - 1)
+                if n == ROUNDS - 1:
+                    exponential(n, 1, 1)
                 add_sums(n - 1)
                 invert_sums(n - 2)
                 if ahead is not None:
                     if 0 < j <= len(STEPS):
                         step = STEPS[j - 1]
-                        keep_inputs(ahead, *step, half_done[ahead], on_vector=(step[0] != [1]))
+                        keep_inputs(ahead, *step, half_done[ahead], on_vector=(step[0] == [0]))
                     if j == 1:
                         group_v(ahead)
                     if j in (3, 4):

from contextlib import ExitStack
import math

import concourse.mybir as mybir
from concourse.masks import make_identity

F32 = mybir.dt.float32
BF16 = mybir.dt.bfloat16
U32 = mybir.dt.uint32
I32 = mybir.dt.int32
U8 = mybir.dt.uint8
FP8X4 = mybir.dt.float8_e4m3fn_x4
ALU = mybir.AluOpType
ACT = mybir.ActivationFunctionType

P = 128
S = 1024
H = 16
HKV = 8
D = 128
TILES = S // P
SLAB = 64
SLABS = S // SLAB
BANK = 512
K_PASS = 512
WORDS = P
SCALE = 1.0 / math.sqrt(D)
MASKED = -1.0e30

JOBS = [
    [(6, 0), (7, WORDS)],
    [(14, 0)],
    [(15, 0)],
    [(8, 0), (4, WORDS + 32)],
    [(9, 0), (5, WORDS + 32)],
    [(10, 0), (2, WORDS + 64)],
    [(11, 0), (3, WORDS + 64)],
    [(12, 0), (0, WORDS + 96)],
    [(13, 0), (1, WORDS + 96)],
]
UNITS = [[14, 15, 6, 7], [8, 9, 4, 5], [10, 11, 2, 3], [12, 13, 0, 1]]
N_JOBS = len(JOBS)
ROUNDS = HKV * N_JOBS

FLOPS = 2 * 2 * D * H * (512 * 512 + 512 * 1024)


def keys_of(slab):
    return (slab + 1) * SLAB


def unit_of(slab):
    for u in range(len(UNITS)):
        if slab in UNITS[u]:
            return u, UNITS[u].index(slab)


def last_job_of(u):
    return max(j for j in range(N_JOBS) for slab, w in JOBS[j] if slab in UNITS[u])


def pieces_of(job):
    pieces = []
    for part in range(len(JOBS[job])):
        slab, w0 = JOBS[job][part]
        start, end = 4 * w0, 4 * w0 + keys_of(slab)
        for bank in range(2):
            lo, hi = max(start, bank * BANK), min(end, (bank + 1) * BANK)
            if lo < hi:
                pieces.append((part, slab, bank, lo - bank * BANK, lo - start, hi - start))
    return pieces


def tile_model_kernel(tc, q, k, v, out):
    nc = tc.nc
    with ExitStack() as ctx:
        const = ctx.enter_context(tc.tile_pool(name="const", bufs=1))
        raw = ctx.enter_context(tc.tile_pool(name="raw", bufs=1))
        strips = ctx.enter_context(tc.tile_pool(name="strips", bufs=1))
        group = ctx.enter_context(tc.tile_pool(name="group", bufs=2))
        work = ctx.enter_context(tc.tile_pool(name="work", bufs=4))
        packed = ctx.enter_context(tc.tile_pool(name="packed", bufs=4))
        results = ctx.enter_context(tc.tile_pool(name="results", bufs=HKV * len(UNITS)))
        s_banks = ctx.enter_context(tc.psum_pool(name="s_banks", bufs=5))
        flip_banks = ctx.enter_context(tc.psum_pool(name="flip_banks", bufs=1))
        pv_banks = ctx.enter_context(tc.psum_pool(name="pv_banks", bufs=1))
        prep_banks = ctx.enter_context(tc.psum_pool(name="prep_banks", bufs=1))

        q_raw = raw.tile([P, HKV, TILES, 2 * D], BF16)
        k_raw = raw.tile([P, HKV, TILES, D], BF16)
        v_raw = raw.tile([P, HKV, 2, 4, D], BF16)
        q_view = q.rearrange("b (t p) h d -> p (b t) (h d)", p=P)
        k_view = k.rearrange("b (t p) h d -> p (b t) (h d)", p=P)
        v_view = v.rearrange("b (c p t) h d -> c p (b t) (h d)", p=P, t=4)

        def load_k(g, t0, t1):
            nc.sync.dma_start(out=k_raw[:, g, t0:t1], in_=k_view[:, t0:t1, g * D : (g + 1) * D])

        def load_q(g, t0, t1):
            nc.sync.dma_start(out=q_raw[:, g, t0:t1], in_=q_view[:, t0:t1, g * 2 * D : (g + 1) * 2 * D])

        def load_v(g):
            for c in range(2):
                nc.sync.dma_start(out=v_raw[:, g, c], in_=v_view[c][:, :, g * D : (g + 1) * D])

        HALF = TILES // 2
        load_k(0, 0, HALF)
        load_q(0, HALF - 1, HALF)
        load_k(0, HALF, TILES)
        load_q(0, HALF, TILES)
        load_v(0)
        load_q(0, 0, HALF - 1)
        load_k(1, 0, TILES)
        load_q(1, 0, TILES)
        load_v(1)

        ident_bf = const.tile([P, P], BF16)
        make_identity(nc, ident_bf[:])
        ident_f32 = const.tile([P, P], F32)
        make_identity(nc, ident_f32[:])
        warm = const.tile([P, 1], F32)
        nc.vector.memset(warm[:], 0.0)
        nc.scalar.activation(out=warm[:], in_=warm[:], func=ACT.Exp)
        mask_f32 = const.tile([P, P], F32)
        nc.gpsimd.memset(mask_f32[:], 0.0)
        nc.gpsimd.affine_select(
            out=mask_f32[:], in_=mask_f32[:], compare_op=ALU.is_ge, fill=MASKED,
            base=0, pattern=[[-1, P]], channel_multiplier=1,
        )
        mask_bf = const.tile([P, SLAB], BF16)
        for hh in range(2):
            part = slice(hh * SLAB, (hh + 1) * SLAB)
            nc.vector.tensor_copy(out=mask_bf[part, :], in_=mask_f32[part, part])

        e_strips = []
        for j in range(N_JOBS):
            strip = strips.tile([P, 2, 2 * 2 * WORDS], BF16, name="e_%d" % j)
            e_strips.append(strip)
            ends = [w0 + keys_of(slab) // 4 for slab, w0 in JOBS[j]]
            starts = [w0 for slab, w0 in JOBS[j][1:]] + [2 * WORDS]
            for lo, hi in zip(ends, starts):
                if lo < hi:
                    nc.vector.memset(strip[:, :, 2 * lo : 2 * hi], 0.0)

        e_sums = {}
        for u in range(len(UNITS)):
            for parity in range(2):
                e_sums[(u, parity)] = strips.tile([P, 4, 2], F32, name="e_sums_%d_%d" % (u, parity))
                nc.gpsimd.memset(e_sums[(u, parity)][:], 0.0)

        VW = D + D // 4
        v_plain = []
        v_part = []
        for parity in range(2):
            plain = strips.tile([P, 2, VW], U32, name="v_plain_%d" % parity, align_bytes=64)
            parts = strips.tile([P, 2, 3, VW], U32, name="v_part_%d" % parity, align_bytes=64)
            nc.gpsimd.memset(plain[:].bitcast(I32), 0)
            nc.gpsimd.memset(parts[:].bitcast(I32), 0)
            v_plain.append(plain)
            v_part.append(parts)

        kT = {}
        qT = {}
        half_done = {}
        v_grouped_of = {}

        def input_block(g, what, t):
            if what == 0:
                return k_raw[:, g, t, :]
            return q_raw[:, g, t, (what - 1) * D : what * D]

        def flip_inputs(g, whats, t0, t1, pool=prep_banks, tag="flipped"):
            flipped = pool.tile([P, len(whats), t1 - t0, P], BF16, tag=tag, name="flipped")
            for i in range(len(whats)):
                for t in range(t0, t1):
                    nc.tensor.transpose(flipped[:, i, t - t0, :], input_block(g, whats[i], t), ident_bf[:])
            return flipped

        def keep_inputs(g, whats, t0, t1, flipped, on_vector):
            if g not in kT:
                kT[g] = group.tile([P, S // 2], F32, name="kT")
                qT[g] = group.tile([P, SLABS, 2, SLAB // 2], F32, name="qT")
            words = flipped[:].rearrange("p w t x -> p (w t x)").bitcast(F32)
            if whats[0] == 0:
                dst = kT[g][:, t0 * P // 2 : t1 * P // 2]
            else:
                dst = qT[g][:, 2 * t0 : 2 * t1, whats[0] - 1 : whats[-1], :]
                words = words.rearrange("p (h i x) -> p i h x", h=len(whats), x=SLAB // 2)
            if on_vector:
                nc.vector.tensor_copy(out=dst, in_=words)
            else:
                nc.scalar.copy(out=dst, in_=words)

        def prepare(g, whats, t0, t1, on_vector):
            flipped = flip_inputs(g, whats, t0, t1, pool=s_banks, tag="bank")
            keep_inputs(g, whats, t0, t1, flipped, on_vector)

        STEPS = [([what], half * TILES // 2, (half + 1) * TILES // 2) for half in range(2) for what in range(3)]

        def group_v(g):
            v_grouped = group.tile([P, 2, D, 4], BF16, align_bytes=64)
            nc.gpsimd.tensor_scalar(
                out=v_grouped[:], in0=v_raw[:, g].rearrange("p c t d -> p c d t"),
                scalar1=1.0, scalar2=0.0, op0=ALU.mult, op1=ALU.add,
            )
            v_grouped_of[g] = v_grouped

        def codes(words):
            return words[:, 0:D].bitcast(FP8X4)

        def scales(words):
            return words[:, D:VW].bitcast(U8)

        def quantise_v(g, c):
            words = v_plain[g % 2][:, c]
            nc.vector.quantize_mx(
                out=codes(words), scales=scales(words), in_=v_grouped_of[g][:, c].rearrange("p d t -> p (d t)")
            )

        def spread_v(g):
            plain = v_plain[g % 2][:].bitcast(I32)
            parts = v_part[g % 2][:].bitcast(I32)
            for x in range(1, 4):
                cut = 32 * x
                nc.sync.dma_start(out=parts[0:cut, 0, x - 1], in_=plain[0:cut, 1])
                nc.sync.dma_start(out=parts[cut:P, 1, x - 1], in_=plain[0 : P - cut, 0])

        s_of = {}
        high_of = {}
        low_of = {}
        short_low_of = {}
        total_of = {}
        recip_of = {}
        flipped_of = {}
        grouped_of = {}
        e_codes = {}
        e_scales = {}
        pv_of = {}

        def live(n):
            return 0 <= n < ROUNDS

        def scores(n, bank):
            if not live(n):
                return
            g, j = divmod(n, N_JOBS)
            if not [piece for piece in pieces_of(j) if piece[2] == bank]:
                return
            s_ps = s_banks.tile([P, BANK], F32, tag="bank", name="s_ps")
            for part, slab, b, col, lo, hi in pieces_of(j):
                if b != bank:
                    continue
                queries = qT[g][:, slab].rearrange("p h x -> p (h x)").bitcast(BF16)
                keys = kT[g][:].bitcast(BF16)
                diagonal = keys_of(slab) - SLAB
                before = min(hi, diagonal) - lo
                if before > 0:
                    nc.tensor.matmul(
                        out=s_ps[:, col : col + before], lhsT=queries, rhs=keys[:, lo : lo + before],
                        start=True, stop=True,
                    )
                if hi > diagonal:
                    at = s_ps[:, col + before : col + before + SLAB]
                    nc.tensor.matmul(out=at, lhsT=ident_bf[:], rhs=mask_bf[:], start=True, stop=False)
                    nc.tensor.matmul(out=at, lhsT=queries, rhs=keys[:, diagonal:hi], start=False, stop=True)
            s_of[(n, bank)] = s_ps

        def row_maximum(n, part, bank):
            if not live(n):
                return
            if n not in high_of:
                high_of[n] = work.tile([P, 2, 2], F32, name="high")
            pieces = [piece for piece in pieces_of(n % N_JOBS) if piece[2] == bank]
            widths = [hi - lo for p, slab, b, col, lo, hi in pieces]
            if len(pieces) == 2 and widths[0] == widths[1]:
                if part == 1:
                    nc.vector.reduce_max(
                        out=high_of[n][:].rearrange("q p c -> q (p c)")[:, 1:3],
                        in_=s_of[(n, bank)][:].rearrange("q (p k) -> q p k", p=2)[:, :, 0 : widths[0]],
                        axis=mybir.AxisListType.X,
                    )
                return
            for p, slab, b, col, lo, hi in pieces:
                if p == part:
                    second = 1 if lo > 0 else 0
                    nc.vector.reduce_max(
                        out=high_of[n][:, p, second : second + 1], in_=s_of[(n, bank)][:, col : col + hi - lo],
                        axis=mybir.AxisListType.X,
                    )

        def bounds(n):
            if not live(n):
                return
            job = JOBS[n % N_JOBS]
            low_of[n] = work.tile([P, 2], F32, name="low")
            high = high_of[n]
            if keys_of(job[0][0]) <= BANK:
                nc.vector.tensor_scalar(out=low_of[n][:], in0=high[:, :, 0], scalar1=-SCALE, scalar2=None, op0=ALU.mult)
                return
            if len(job) > 1:
                short_low_of[n] = work.tile([P, 1], F32, name="short_low")
                nc.gpsimd.tensor_scalar(
                    out=short_low_of[n][:], in0=high[:, 1, 0:1], scalar1=-SCALE, scalar2=0.0, op0=ALU.mult, op1=ALU.add
                )
            nc.vector.tensor_scalar(
                out=low_of[n][:, 0:1], in0=high[:, 0, 0:1],
                scalar1=high[:, 0, 1:2], scalar2=-SCALE, op0=ALU.max, op1=ALU.mult,
            )

        def exponential(n, part, bank):
            if not live(n):
                return
            g, j = divmod(n, N_JOBS)
            for p, slab, b, col, lo, hi in pieces_of(j):
                if (p, b) != (part, bank):
                    continue
                w0 = JOBS[j][p][1] + lo // 4
                words = (hi - lo) // 4
                u, place = unit_of(slab)
                second = 1 if lo > 0 else 0
                low = short_low_of[n][:] if p == 1 and n in short_low_of else low_of[n][:, p : p + 1]
                nc.scalar.activation(
                    out=e_strips[j][:, :, 2 * w0 : 2 * (w0 + words)].rearrange("q u (m i) -> q u m i", i=2),
                    in_=s_of[(n, bank)][:, col : col + hi - lo].rearrange("q (m u i) -> q u m i", u=2, i=2),
                    func=ACT.Exp, bias=low, scale=SCALE,
                    accum_out=e_sums[(u, g % 2)][:, place, second : second + 1],
                )

        def transposes(n):
            if not live(n):
                return
            words = e_strips[n % N_JOBS][:].bitcast(F32)
            flipped = flip_banks.tile([P, 2, 2, P], F32, name="e_flipped")
            for a in range(2):
                for u in range(2):
                    nc.tensor.transpose(flipped[:, a, u, :], words[:, u, a * WORDS : (a + 1) * WORDS], ident_f32[:])
            flipped_of[n] = flipped

        def regroup(n):
            if not live(n):
                return
            grouped = work.tile([P, 2 * 4 * P], BF16, align_bytes=64)
            nc.scalar.copy(
                out=grouped[:].bitcast(F32).rearrange("p (a r u) -> p a r u", a=2, u=2),
                in_=flipped_of[n][:].rearrange("p a u r -> p a r u"),
            )
            grouped_of[n] = grouped

        def quantise(n):
            if not live(n):
                return
            e_codes[n] = packed.tile([P, 2 * P], U32, name="e_codes", align_bytes=64)
            e_scales[n] = packed.tile([P, 2 * P], U8, name="e_scales", align_bytes=64)
            nc.vector.quantize_mx(out=e_codes[n][:].bitcast(FP8X4), scales=e_scales[n][:], in_=grouped_of[n][:])

        def v_operands(g, j, part):
            slab, w0 = JOBS[j][part]
            plain = v_plain[g % 2]
            parts = v_part[g % 2]
            if slab < SLABS // 2:
                a, q0 = divmod(w0, WORDS)
                return [(a, plain[:, 0] if q0 == 0 else parts[:, 1, q0 // 32 - 1])]
            if len(JOBS[j]) == 1:
                return [(0, plain[:, 0]), (1, plain[:, 1])]
            cut = JOBS[j][1][1] - WORDS
            return [(0, plain[:, 0]), (1, parts[:, 0, cut // 32 - 1])]

        def weighted_sums(n):
            if not live(n):
                return
            g, j = divmod(n, N_JOBS)
            for part in range(len(JOBS[j])):
                u, place = unit_of(JOBS[j][part][0])
                if (g, u) not in pv_of:
                    pv_of[(g, u)] = pv_banks.tile([P, 4, D], F32, name="pv")
                passes = v_operands(g, j, part)
                for i in range(len(passes)):
                    a, words = passes[i]
                    nc.tensor.matmul_mx(
                        out=pv_of[(g, u)][:, place, :],
                        lhsT=e_codes[n][:, a * P : (a + 1) * P].bitcast(FP8X4),
                        lhsT_scale=e_scales[n][:, a * P : (a + 1) * P],
                        rhs=codes(words),
                        rhs_scale=scales(words),
                        start=(i == 0),
                        stop=(i == len(passes) - 1),
                    )

        def finished_by(n):
            if not live(n):
                return []
            g, j = divmod(n, N_JOBS)
            return [(g, u) for u in range(len(UNITS)) if last_job_of(u) == j]

        def add_sums(n):
            for g, u in finished_by(n):
                sums = e_sums[(u, g % 2)]
                total_of[(g, u)] = work.tile([P, 4], F32, name="total")
                nc.gpsimd.tensor_tensor(out=total_of[(g, u)][:], in0=sums[:, :, 0], in1=sums[:, :, 1], op=ALU.add)

        def invert_sums(n):
            for gu in finished_by(n):
                recip_of[gu] = work.tile([P, 4], F32, name="recip")
                nc.vector.reciprocal(out=recip_of[gu][:], in_=total_of[gu][:])

        def normalise(n):
            for gu in finished_by(n):
                g, u = gu
                o_sb = results.tile([P, 4, D], F32)
                nc.vector.tensor_tensor(
                    out=o_sb[:], in0=pv_of[gu][:], in1=recip_of[gu][:].unsqueeze(2).to_broadcast([P, 4, D]), op=ALU.mult
                )
                for pair in range(2):
                    first = UNITS[u][2 * pair] * SLAB
                    for hh in range(2):
                        nc.sync.dma_start(
                            out=out[0, first : first + 2 * SLAB, 2 * g + hh, :].rearrange("(i x) d -> x i d", x=SLAB),
                            in_=o_sb[hh * SLAB : (hh + 1) * SLAB, 2 * pair : 2 * pair + 2, :],
                        )

        with tc.manual_schedule():
            prepare(0, [0], 0, HALF, on_vector=True)
            prepare(0, [1, 2], HALF - 1, HALF, on_vector=False)
            prepare(0, [0], HALF, TILES, on_vector=True)
            for n in range(-2, ROUNDS + 4):
                g, j = divmod(n, N_JOBS)
                ahead = g + 1 if 0 <= g < HKV - 1 else None
                if j == 0 and 0 <= g < HKV - 2:
                    load_k(g + 2, 0, TILES)
                    load_q(g + 2, 0, TILES)
                    load_v(g + 2)
                scores(n + 2, 0)
                row_maximum(n + 1, 0, 0)
                normalise(n - 4)
                row_maximum(n + 1, 1, 1)
                row_maximum(n + 1, 0, 1)
                exponential(n, 0, 0)
                exponential(n, 0, 1)
                if n < ROUNDS - 1:
                    exponential(n, 1, 1)
                transposes(n - 1)
                if ahead is not None and 0 < j <= len(STEPS):
                    half_done[ahead] = flip_inputs(ahead, *STEPS[j - 1])
                weighted_sums(n - 3)
                scores(n + 2, 1)
                quantise(n - 2)
                bounds(n + 1)
                regroup(n - 1)
                if n == ROUNDS - 1:
                    exponential(n, 1, 1)
                add_sums(n - 1)
                invert_sums(n - 2)
                if ahead is not None:
                    if 0 < j <= len(STEPS):
                        step = STEPS[j - 1]
                        keep_inputs(ahead, *step, half_done[ahead], on_vector=(step[0] == [0]))
                    if j == 1:
                        group_v(ahead)
                    if j in (3, 4):
                        quantise_v(ahead, j - 3)
                    if j == 5:
                        spread_v(ahead)
                if n == -2:
                    prepare(0, [1], HALF, TILES, on_vector=False)
                    prepare(0, [2], HALF, TILES, on_vector=False)
                    group_v(0)
                if n == -1:
                    quantise_v(0, 0)
                    quantise_v(0, 1)
                    spread_v(0)
                if n == 0:
                    flipped = flip_inputs(0, [1, 2], 0, HALF - 1)
                    keep_inputs(0, [1, 2], 0, HALF - 1, flipped, on_vector=False)
